import numpy as np
import ml_dtypes


def mxq(x, axis, fmt="e4m3"):
    dtype, down = {"e4m3": (ml_dtypes.float8_e4m3fn, 7), "e5m2": (ml_dtypes.float8_e5m2, 14)}[fmt]
    v = np.moveaxis(np.asarray(x, np.float32).astype(ml_dtypes.bfloat16).astype(np.float64), axis, -1)
    blocks = v.reshape(v.shape[:-1] + (-1, 32))
    amax = np.abs(blocks).max(-1, keepdims=True)
    byte = np.maximum(np.where(amax > 0, np.frexp(amax)[1] - 1 + 127, 0) - down, 1)
    scale = np.exp2(byte - 127.0)
    codes = (blocks / scale).astype(np.float32).astype(dtype).astype(np.float64)
    return np.moveaxis((codes * scale).reshape(v.shape), -1, axis)


WIDE = False


def mx_kscale(k):
    if not WIDE:
        return np.ones(k)
    levels = np.array([18, -18])
    if k % 512:
        return np.exp2(np.random.permutation(np.resize(levels, k // 32))).repeat(32)
    a = np.empty((k // 512, 16))
    for p in range(k // 512):
        a[p, :8] = np.random.permutation(np.resize(levels, 8))
        for g in range(8):
            far = levels[np.abs(levels - a[p, g]) >= 10]
            a[p, g + 8] = far[np.random.randint(len(far))]
    return np.exp2(a.ravel()).repeat(32)


BF16 = ml_dtypes.bfloat16


def bf(x):
    return np.asarray(x, np.float32).astype(BF16)


def f64(x):
    return np.asarray(x).astype(np.float64)


NB, D, CO, CV, R = 16, 512, 128, 512, 512
N = NB * CO


def setup_inputs():
    s = mx_kscale(N).reshape(NB, 1, CO)
    u = mx_kscale(D)
    v = mx_kscale(R)
    x1_0 = bf(np.random.standard_normal((NB, D, CO)))
    A_0 = bf(np.random.standard_normal((D, R)) / np.sqrt(D))
    t2 = bf(np.random.standard_normal((NB, R, CV)))
    w = bf(np.random.standard_normal((NB, CO, CV)) / np.sqrt(CV))
    C_0 = bf(np.random.standard_normal((D, R)) / np.sqrt(R))
    g = bf(np.random.standard_normal((NB, D, CO)) * np.exp2(np.random.randint(-6, 1, (NB, 1, CO))) / s * u[None, :, None])
    t3 = f64(t2) @ f64(w).transpose(0, 2, 1)
    return {"x1": bf(f64(x1_0) * s), "A": bf(f64(A_0) / v), "t2": t2, "w": w,
            "C": bf(f64(C_0) * v / u[:, None]), "t3": np.asarray(t3, np.float32), "grad_out": g}


def flat_tokens(a):
    return a.transpose(1, 0, 2).reshape(a.shape[1], N)


def reference(x1, A, t2, w, C, t3, grad_out):
    g = flat_tokens(f64(grad_out))
    dh = mxq(f64(C), 0, "e4m3").T @ mxq(g, 0, "e5m2")
    dt1 = dh * flat_tokens(f64(t3))
    dx = mxq(f64(A), 1, "e4m3") @ mxq(dt1, 0, "e5m2")
    dA = mxq(flat_tokens(f64(x1)), 1, "e4m3") @ mxq(dt1, 1, "e5m2").T
    return dx.reshape(D, NB, CO).transpose(1, 0, 2), dA

@@ -1,0 +1,366 @@
+from contextlib import ExitStack
+
+import concourse.mybir as mybir
+from concourse.masks import make_identity
+
+NB, D, CO, R = 16, 512, 128, 512
+N = NB * CO
+FLOPS = 3 * 2 * D * R * N
+BYTES = 2 * (2 * NB * D * CO + 2 * D * R) + 4 * (2 * NB * D * CO + D * R)
+
+P = 128
+J = 4
+G = 4
+B = 4
+NT = B * CO
+
+F32 = mybir.dt.float32
+BF16 = mybir.dt.bfloat16
+U32 = mybir.dt.uint32
+U8 = mybir.dt.uint8
+E4 = mybir.dt.float8_e4m3fn_x4
+E5 = mybir.dt.float8_e5m2_x4
+MULT = mybir.AluOpType.mult
+
+
+def tile_cptensorproduct_pa_v_kernel(tc, x1, A, t2, w, C, t3, grad_out, out_0, out_1):
+    nc = tc.nc
+    with ExitStack() as ctx:
+        keep = ctx.enter_context(tc.tile_pool(name="keep", bufs=1))
+        ring = ctx.enter_context(tc.tile_pool(name="ring", bufs=2))
+        outs = ctx.enter_context(tc.tile_pool(name="outs", bufs=4))
+        psum = ctx.enter_context(tc.psum_pool(name="psum", bufs=1))
+        ctx.enter_context(tc.manual_schedule())
+
+        def bank(k):
+            return psum.tile([P, 512], F32, name="bank%d" % k, tag="bank%d" % k)
+
+        def raw(name, dtype):
+            return keep.tile([P, B, J, CO], dtype, name=name, align_bytes=64)
+
+        def codes(name):
+            return (
+                keep.tile([P, 512], U32, name=name + "_codes", align_bytes=64),
+                keep.tile([P, 512], U8, name=name + "_scales", align_bytes=64),
+            )
+
+        g_raw = [raw("g_raw%d" % i, BF16) for i in range(G)]
+        x_raw = [keep.tile([P, J, B, CO], BF16, name="x_raw%d" % i, align_bytes=64) for i in range(G)]
+        t3_raw = [raw("t3_raw%d" % i, F32) for i in range(G)]
+        c_raw = keep.tile([P, J, R], BF16, name="c_raw", align_bytes=64)
+        a_raw = keep.tile([P, J, R], BF16, name="a_raw", align_bytes=64)
+
+        def load_group(tile, src, i):
+            nc.sync.dma_start(
+                out=tile[:].rearrange("p b j c -> p b (j c)"),
+                in_=src[B * i : B * (i + 1)].rearrange("b (p j) c -> p b (j c)", j=J),
+            )
+
+        def load_pair(tile, src, i, h):
+            nc.sync.dma_start(
+                out=tile[:, 2 * h : 2 * h + 2].rearrange("p b j c -> p b (j c)"),
+                in_=src[B * i + 2 * h : B * i + 2 * h + 2].rearrange("b (p j) c -> p b (j c)", j=J),
+            )
+
+        def load_x(i):
+            for b in range(B):
+                nc.sync.dma_start(
+                    out=x_raw[i][:, :, b, :], in_=x1[B * i + b].rearrange("(p j) c -> p j c", j=J)
+                )
+
+        c_view = C.rearrange("(p j) r -> p j r", j=J)
+        for h in range(2):
+            nc.sync.dma_start(out=c_raw[:, :, 256 * h : 256 * (h + 1)], in_=c_view[:, :, 256 * h : 256 * (h + 1)])
+        load_pair(g_raw[0], grad_out, 0, 0)
+        load_pair(g_raw[0], grad_out, 0, 1)
+        def load_t3_half(h):
+            view = t3[0:B].rearrange("b (p j) c -> p b j c", j=J)
+            nc.sync.dma_start(out=t3_raw[0][:, :, 2 * h : 2 * h + 2, :], in_=view[:, :, 2 * h : 2 * h + 2, :])
+
+        load_t3_half(0)
+        nc.sync.dma_start(out=a_raw[:], in_=A.rearrange("(p j) r -> p j r", j=J))
+        load_t3_half(1)
+        load_group(g_raw[1], grad_out, 1)
+        load_x(0)
+        load_group(t3_raw[1], t3, 1)
+        load_group(g_raw[2], grad_out, 2)
+        load_x(1)
+        load_group(t3_raw[2], t3, 2)
+        load_group(g_raw[3], grad_out, 3)
+        load_x(2)
+        load_group(t3_raw[3], t3, 3)
+        load_x(3)
+
+        ident = keep.tile([P, P], F32, name="ident")
+        make_identity(nc, ident[:])
+
+        c_q = codes("c")
+        a_q = codes("a")
+        g_q = [codes("g%d" % i) for i in range(G)]
+        x_q = [codes("x%d" % i) for i in range(G)]
+        r_q = [codes("r%d" % i) for i in range(G)]
+        n_q = [codes("n%d" % i) for i in range(G)]
+
+        def quantize(q, grouped, fmt):
+            nc.vector.quantize_mx(out=q[0][:].bitcast(fmt), scales=q[1][:], in_=grouped)
+
+        def mm(out, lhs, col, lfmt, rhs, rfmt, start, stop):
+            nc.tensor.matmul_mx(
+                out=out[:],
+                lhsT=lhs[0][:, P * col : P * (col + 1)].bitcast(lfmt),
+                lhsT_scale=lhs[1][:, P * col : P * (col + 1)],
+                rhs=rhs[0][:].bitcast(rfmt),
+                rhs_scale=rhs[1][:],
+                start=start,
+                stop=stop,
+            )
+
+        def tcopy(eng, out, in_):
+            if eng == "S":
+                nc.scalar.copy(out=out, in_=in_)
+            else:
+                nc.vector.tensor_copy(out=out, in_=in_)
+
+        c_grp = keep.tile([P, R * J], BF16, name="c_grp", align_bytes=64)
+
+        def c_int(h, eng):
+            tcopy(
+                eng,
+                c_grp[:].rearrange("p (t m j) -> p t m j", t=J, j=J)[:, :, 64 * h : 64 * (h + 1), :],
+                c_raw[:, :, 256 * h : 256 * (h + 1)].rearrange("p j (m t) -> p t m j", t=J),
+            )
+
+        g_grp = {}
+
+        def g_int(i, b, eng):
+            if i not in g_grp:
+                g_grp[i] = ring.tile([P, NT, J], BF16, name="g_grp", align_bytes=64)
+            tcopy(
+                eng,
+                g_grp[i][:, CO * b : CO * (b + 1), :].rearrange("p (c k) j -> p c j k", k=4),
+                g_raw[i][:, b].rearrange("p j (c k) -> p c j k", k=4),
+            )
+
+        def g_quant(i, h=None):
+            flat = g_grp[i][:].rearrange("p n j -> p (n j)")
+            if h is None:
+                quantize(g_q[i], flat, E5)
+            else:
+                nc.vector.quantize_mx(
+                    out=g_q[i][0][:, 256 * h : 256 * (h + 1)].bitcast(E5),
+                    scales=g_q[i][1][:, 256 * h : 256 * (h + 1)],
+                    in_=flat[:, 1024 * h : 1024 * (h + 1)],
+                )
+
+        dh = {}
+
+        def dh_mm(i):
+            for t in range(J):
+                dh[i, t] = bank((t + 2 * (i % 2)) % 4)
+                mm(dh[i, t], c_q, t, E4, g_q[i], E5, True, True)
+
+        dt1 = {}
+
+        def mul(i, t):
+            if t == 0:
+                dt1[i] = ring.tile([P, J, NT], BF16, name="dt1", align_bytes=64)
+            nc.vector.tensor_tensor(
+                out=dt1[i][:, t, :].rearrange("p (b c) -> p b c", b=B),
+                in0=dh[i, t][:].rearrange("p (b c) -> p b c", b=B),
+                in1=t3_raw[i][:, :, t, :],
+                op=MULT,
+            )
+
+        d_int_tile = {}
+
+        def d_int(i, q, eng):
+            if i not in d_int_tile:
+                d_int_tile[i] = ring.tile([P, NT, J], BF16, name="dt1_grp", align_bytes=64)
+            cols = slice(CO * q[0], CO * q[1])
+            tcopy(
+                eng,
+                d_int_tile[i][:, cols, :].rearrange("p (c k) t -> p c t k", k=4),
+                dt1[i][:, :, cols].rearrange("p t (c k) -> p c t k", k=4),
+            )
+
+        def r_quant(i):
+            quantize(r_q[i], d_int_tile[i][:].rearrange("p n t -> p (n t)"), E5)
+
+        def transposes(words, contiguous, h, tr):
+            for s in range(2):
+                for u in range(2):
+                    base = 256 * (2 * h + s)
+                    if contiguous:
+                        src = words[:, base + P * u : base + P * (u + 1)]
+                    else:
+                        src = words[:, base + u : base + 256 : 2]
+                    nc.tensor.transpose(tr[:, 256 * s + P * u : 256 * s + P * (u + 1)], src, ident[:])
+
+        def tr_copy(eng, grouped, h, tr):
+            tcopy(
+                eng,
+                grouped[:].bitcast(F32)[:, 512 * h : 512 * (h + 1)].rearrange("p (s k u) -> p s k u", s=2, u=2),
+                tr[:].rearrange("p (s u k) -> p s k u", s=2, u=2),
+            )
+
+        n_tr, n_grp = {}, {}
+
+        def n_tp(i, h):
+            n_tr[i, h] = bank(h + 2 * (i % 2))
+            transposes(dt1[i][:].rearrange("p t n -> p (t n)").bitcast(F32), False, h, n_tr[i, h])
+
+        def n_cp(i, h, eng):
+            if h == 0:
+                n_grp[i] = ring.tile([P, 2048], BF16, name="n_grp", align_bytes=64)
+            tr_copy(eng, n_grp[i], h, n_tr[i, h])
+
+        def n_quant(i):
+            quantize(n_q[i], n_grp[i][:], E5)
+
+        x_tr, x_grp = {}, {}
+
+        def x_tp(i, h, k=4):
+            x_tr[i, h] = bank(k + h)
+            transposes(x_raw[i][:].rearrange("p j b c -> p (j b c)").bitcast(F32), False, h, x_tr[i, h])
+
+        def x_cp(i, h, eng):
+            if h == 0:
+                x_grp[i] = ring.tile([P, 2048], BF16, name="x_grp", align_bytes=64)
+            tr_copy(eng, x_grp[i], h, x_tr[i, h])
+
+        def x_quant(i):
+            quantize(x_q[i], x_grp[i][:], E4)
+
+        a_tr = {}
+        a_grp = keep.tile([P, 2048], BF16, name="a_grp", align_bytes=64)
+
+        def a_tp(h):
+            a_tr[h] = bank(6 + h)
+            transposes(a_raw[:].rearrange("p j r -> p (j r)").bitcast(F32), False, h, a_tr[h])
+
+        def a_cp(h, eng):
+            tr_copy(eng, a_grp, h, a_tr[h])
+
+        def a_quant():
+            quantize(a_q, a_grp[:], E4)
+
+        dx, dx_sb = {}, {}
+
+        def dx_mm(i, j, k):
+            dx[i, j] = bank(k)
+            mm(dx[i, j], a_q, j, E4, r_q[i], E5, True, True)
+
+        def dx_cp(i, j, eng):
+            if i not in dx_sb:
+                dx_sb[i] = outs.tile([P, B, J, CO], F32, name="dx_sb", align_bytes=64)
+            tcopy(eng, dx_sb[i][:, :, j, :], dx[i, j][:].rearrange("p (b c) -> p b c", b=B))
+
+        def dx_store(i, j0, j1):
+            nc.sync.dma_start(
+                out=out_0[B * i : B * (i + 1)].rearrange("b (p j) c -> p b j c", j=J)[:, :, j0:j1, :].rearrange("p b j c -> p b (j c)") if j1 - j0 == J else out_0[B * i : B * (i + 1)].rearrange("b (p j) c -> p b j c", j=J)[:, :, j0:j1, :],
+                in_=dx_sb[i][:].rearrange("p b j c -> p b (j c)") if j1 - j0 == J else dx_sb[i][:, :, j0:j1, :],
+            )
+
+        da = {}
+        da_sb = keep.tile([P, J, R], F32, name="da_sb", align_bytes=64)
+
+        def da_open(j, k):
+            da[j] = bank(k)
+
+        def da_mm(i, j):
+            mm(da[j], x_q[i], j, E4, n_q[i], E5, i == 0, i == G - 1)
+
+        def da_cp(j, eng):
+            tcopy(
+                eng,
+                da_sb[:, j, :].rearrange("p (m t) -> p m t", t=J),
+                da[j][:].rearrange("p (t m) -> p m t", t=J),
+            )
+            nc.sync.dma_start(out=out_1.rearrange("(p j) r -> p j r", j=J)[:, j, :], in_=da_sb[:, j, :])
+
+        c_int(0, "V")
+        c_int(1, "V")
+        quantize(c_q, c_grp[:], E4)
+        for b in range(B):
+            g_int(0, b, "SSVV"[b])
+        g_quant(0, 0)
+        g_quant(0, 1)
+        dh_mm(0)
+        for h in range(2):
+            a_tp(h)
+        for h in range(2):
+            a_cp(h, "SS"[h])
+        da_open(0, 6)
+        da_open(1, 7)
+        for i in range(G):
+            last = i == G - 1
+            if i > 0:
+                dx_mm(i - 1, 2, 4)
+                dx_mm(i - 1, 3, 5)
+                dx_cp(i - 1, 2, "S")
+                dx_cp(i - 1, 3, "S")
+                dx_store(i - 1, 0, J)
+            if not last:
+                who = ["SSSV", "SSSV", "SSSV"][i]
+                for b in range(B):
+                    if who[b] == "S":
+                        g_int(i + 1, b, "S")
+            for t in range(J):
+                mul(i, t)
+                if t % 2 == 1:
+                    n_tp(i, t // 2)
+            for h in range(2):
+                n_cp(i, h, "S")
+            if last:
+                break
+            for h in range(2):
+                x_tp(i, h)
+            if i == 0:
+                a_quant()
+            for b in range(B):
+                if who[b] == "V":
+                    g_int(i + 1, b, "V")
+            if 0 < i:
+                n_quant(i - 1)
+            d_int(i, (0, 4), "V")
+            for h in range(2):
+                x_cp(i, h, "S")
+            if 0 < i:
+                x_quant(i - 1)
+                da_mm(i - 1, 0)
+                da_mm(i - 1, 1)
+            g_quant(i + 1)
+            dh_mm(i + 1)
+            r_quant(i)
+            dx_mm(i, 0, 4)
+            dx_mm(i, 1, 5)
+            dx_cp(i, 0, "S")
+            dx_cp(i, 1, "S")
+        i = G - 1
+        for h in range(2):
+            x_tp(i, h, 0)
+        pass
+        d_int(i, (0, 4), "V")
+        for h in range(2):
+            x_cp(i, h, "SS"[h])
+        for j in (2, 3):
+            da_open(j, j)
+            for k in range(G - 2):
+                da_mm(k, j)
+        pass
+        r_quant(i)
+        for j in range(J):
+            dx_mm(i, j, (4, 5, 0, 1)[j])
+        n_quant(i - 1)
+        x_quant(i - 1)
+        for j in range(J):
+            da_mm(i - 1, j)
+        n_quant(i)
+        x_quant(i)
+        for j in range(J):
+            dx_cp(i, j, "SSSS"[j])
+            if j % 2 == 1:
+                dx_store(i, j - 1, j + 1)
+        for j in range(J):
+            da_mm(i, j)
+            da_cp(j, "VSVS"[j])

@@ -69,24 +69,27 @@ def tile_cptensorproduct_pa_v_kernel(tc, x1, A, t2, w, C, t3, grad_out, out_0, o
                 )
 
         c_view = C.rearrange("(p j) r -> p j r", j=J)
-        for h in range(2):
+        def load_c(h):
             nc.sync.dma_start(out=c_raw[:, :, 256 * h : 256 * (h + 1)], in_=c_view[:, :, 256 * h : 256 * (h + 1)])
-        load_pair(g_raw[0], grad_out, 0, 0)
-        load_pair(g_raw[0], grad_out, 0, 1)
+
         def load_t3_half(h):
             view = t3[0:B].rearrange("b (p j) c -> p b j c", j=J)
             nc.sync.dma_start(out=t3_raw[0][:, :, 2 * h : 2 * h + 2, :], in_=view[:, :, 2 * h : 2 * h + 2, :])
 
-        load_t3_half(0)
-        nc.sync.dma_start(out=a_raw[:], in_=A.rearrange("(p j) r -> p j r", j=J))
-        load_t3_half(1)
+        load_c(0)
+        load_c(1)
+        load_pair(g_raw[0], grad_out, 0, 1)
         load_group(g_raw[1], grad_out, 1)
-        load_x(0)
-        load_group(t3_raw[1], t3, 1)
+        load_pair(g_raw[0], grad_out, 0, 0)
+        nc.sync.dma_start(out=a_raw[:], in_=A.rearrange("(p j) r -> p j r", j=J))
+        load_t3_half(0)
+        load_t3_half(1)
         load_group(g_raw[2], grad_out, 2)
         load_x(1)
-        load_group(t3_raw[2], t3, 2)
+        load_group(t3_raw[1], t3, 1)
         load_group(g_raw[3], grad_out, 3)
+        load_group(t3_raw[2], t3, 2)
+        load_x(0)
         load_x(2)
         load_group(t3_raw[3], t3, 3)
         load_x(3)
@@ -134,7 +137,7 @@ def tile_cptensorproduct_pa_v_kernel(tc, x1, A, t2, w, C, t3, grad_out, out_0, o
 
         def g_int(i, b, eng):
             if i not in g_grp:
-                g_grp[i] = ring.tile([P, NT, J], BF16, name="g_grp", align_bytes=64)
+                g_grp[i] = ring.tile([P, NT, J], BF16, name="g_grp", align_bytes=64, bufs=3)
             tcopy(
                 eng,
                 g_grp[i][:, CO * b : CO * (b + 1), :].rearrange("p (c k) j -> p c j k", k=4),
@@ -154,15 +157,14 @@ def tile_cptensorproduct_pa_v_kernel(tc, x1, A, t2, w, C, t3, grad_out, out_0, o
 
         dh = {}
 
-        def dh_mm(i):
-            for t in range(J):
-                dh[i, t] = bank((t + 2 * (i % 2)) % 4)
-                mm(dh[i, t], c_q, t, E4, g_q[i], E5, True, True)
+        def dh_mm(i, t, k):
+            dh[i, t] = bank(k)
+            mm(dh[i, t], c_q, t, E4, g_q[i], E5, True, True)
 
         dt1 = {}
 
         def mul(i, t):
-            if t == 0:
+            if i not in dt1:
                 dt1[i] = ring.tile([P, J, NT], BF16, name="dt1", align_bytes=64)
             nc.vector.tensor_tensor(
                 out=dt1[i][:, t, :].rearrange("p (b c) -> p b c", b=B),
@@ -205,13 +207,13 @@ def tile_cptensorproduct_pa_v_kernel(tc, x1, A, t2, w, C, t3, grad_out, out_0, o
 
         n_tr, n_grp = {}, {}
 
-        def n_tp(i, h):
-            n_tr[i, h] = bank(h + 2 * (i % 2))
+        def n_tp(i, h, k):
+            n_tr[i, h] = bank(k)
             transposes(dt1[i][:].rearrange("p t n -> p (t n)").bitcast(F32), False, h, n_tr[i, h])
 
         def n_cp(i, h, eng):
-            if h == 0:
-                n_grp[i] = ring.tile([P, 2048], BF16, name="n_grp", align_bytes=64)
+            if i not in n_grp:
+                n_grp[i] = ring.tile([P, 2048], BF16, name="n_grp", align_bytes=64, bufs=4)
             tr_copy(eng, n_grp[i], h, n_tr[i, h])
 
         def n_quant(i):
@@ -219,13 +221,13 @@ def tile_cptensorproduct_pa_v_kernel(tc, x1, A, t2, w, C, t3, grad_out, out_0, o
 
         x_tr, x_grp = {}, {}
 
-        def x_tp(i, h, k=4):
-            x_tr[i, h] = bank(k + h)
+        def x_tp(i, h, k):
+            x_tr[i, h] = bank(k)
             transposes(x_raw[i][:].rearrange("p j b c -> p (j b c)").bitcast(F32), False, h, x_tr[i, h])
 
         def x_cp(i, h, eng):
-            if h == 0:
-                x_grp[i] = ring.tile([P, 2048], BF16, name="x_grp", align_bytes=64)
+            if i not in x_grp:
+                x_grp[i] = ring.tile([P, 2048], BF16, name="x_grp", align_bytes=64, bufs=4)
             tr_copy(eng, x_grp[i], h, x_tr[i, h])
 
         def x_quant(i):
@@ -234,8 +236,8 @@ def tile_cptensorproduct_pa_v_kernel(tc, x1, A, t2, w, C, t3, grad_out, out_0, o
         a_tr = {}
         a_grp = keep.tile([P, 2048], BF16, name="a_grp", align_bytes=64)
 
-        def a_tp(h):
-            a_tr[h] = bank(6 + h)
+        def a_tp(h, k):
+            a_tr[h] = bank(k)
             transposes(a_raw[:].rearrange("p j r -> p (j r)").bitcast(F32), False, h, a_tr[h])
 
         def a_cp(h, eng):
@@ -264,11 +266,14 @@ def tile_cptensorproduct_pa_v_kernel(tc, x1, A, t2, w, C, t3, grad_out, out_0, o
         da = {}
         da_sb = keep.tile([P, J, R], F32, name="da_sb", align_bytes=64)
 
-        def da_open(j, k):
-            da[j] = bank(k)
+        da_done = {}
 
-        def da_mm(i, j):
-            mm(da[j], x_q[i], j, E4, n_q[i], E5, i == 0, i == G - 1)
+        def da_mm(i, j, k=None):
+            if j not in da:
+                da[j] = bank(k)
+                da_done[j] = 0
+            mm(da[j], x_q[i], j, E4, n_q[i], E5, da_done[j] == 0, da_done[j] == G - 1)
+            da_done[j] += 1
 
         def da_cp(j, eng):
             tcopy(
@@ -276,91 +281,177 @@ def tile_cptensorproduct_pa_v_kernel(tc, x1, A, t2, w, C, t3, grad_out, out_0, o
                 da_sb[:, j, :].rearrange("p (m t) -> p m t", t=J),
                 da[j][:].rearrange("p (t m) -> p m t", t=J),
             )
+
+        def da_store(j):
             nc.sync.dma_start(out=out_1.rearrange("(p j) r -> p j r", j=J)[:, j, :], in_=da_sb[:, j, :])
 
-        c_int(0, "V")
-        c_int(1, "V")
-        quantize(c_q, c_grp[:], E4)
-        for b in range(B):
-            g_int(0, b, "SSVV"[b])
-        g_quant(0, 0)
+        c_int(0, "S")
+        g_int(0, 3, "V")
+        g_int(0, 2, "S")
+        c_int(1, "S")
         g_quant(0, 1)
-        dh_mm(0)
-        for h in range(2):
-            a_tp(h)
-        for h in range(2):
-            a_cp(h, "SS"[h])
-        da_open(0, 6)
-        da_open(1, 7)
-        for i in range(G):
-            last = i == G - 1
-            if i > 0:
-                dx_mm(i - 1, 2, 4)
-                dx_mm(i - 1, 3, 5)
-                dx_cp(i - 1, 2, "S")
-                dx_cp(i - 1, 3, "S")
-                dx_store(i - 1, 0, J)
-            if not last:
-                who = ["SSSV", "SSSV", "SSSV"][i]
-                for b in range(B):
-                    if who[b] == "S":
-                        g_int(i + 1, b, "S")
-            for t in range(J):
-                mul(i, t)
-                if t % 2 == 1:
-                    n_tp(i, t // 2)
-            for h in range(2):
-                n_cp(i, h, "S")
-            if last:
-                break
-            for h in range(2):
-                x_tp(i, h)
-            if i == 0:
-                a_quant()
-            for b in range(B):
-                if who[b] == "V":
-                    g_int(i + 1, b, "V")
-            if 0 < i:
-                n_quant(i - 1)
-            d_int(i, (0, 4), "V")
-            for h in range(2):
-                x_cp(i, h, "S")
-            if 0 < i:
-                x_quant(i - 1)
-                da_mm(i - 1, 0)
-                da_mm(i - 1, 1)
-            g_quant(i + 1)
-            dh_mm(i + 1)
-            r_quant(i)
-            dx_mm(i, 0, 4)
-            dx_mm(i, 1, 5)
-            dx_cp(i, 0, "S")
-            dx_cp(i, 1, "S")
-        i = G - 1
-        for h in range(2):
-            x_tp(i, h, 0)
-        pass
-        d_int(i, (0, 4), "V")
-        for h in range(2):
-            x_cp(i, h, "SS"[h])
-        for j in (2, 3):
-            da_open(j, j)
-            for k in range(G - 2):
-                da_mm(k, j)
-        pass
-        r_quant(i)
-        for j in range(J):
-            dx_mm(i, j, (4, 5, 0, 1)[j])
-        n_quant(i - 1)
-        x_quant(i - 1)
-        for j in range(J):
-            da_mm(i - 1, j)
-        n_quant(i)
-        x_quant(i)
-        for j in range(J):
-            dx_cp(i, j, "SSSS"[j])
-            if j % 2 == 1:
-                dx_store(i, j - 1, j + 1)
-        for j in range(J):
-            da_mm(i, j)
-            da_cp(j, "VSVS"[j])
+        g_int(0, 0, "V")
+        g_int(0, 1, "S")
+        g_int(1, 3, "V")
+        g_int(1, 0, "S")
+        quantize(c_q, c_grp[:], E4)
+        g_quant(0, 0)
+        g_int(1, 1, "S")
+        dh_mm(0, 0, 0)
+        g_int(1, 2, "S")
+        dh_mm(0, 3, 1)
+        mul(0, 0)
+        dh_mm(0, 2, 2)
+        g_quant(1)
+        dh_mm(0, 1, 3)
+        a_tp(0, 4)
+        mul(0, 3)
+        mul(0, 1)
+        dh_mm(1, 2, 5)
+        a_cp(0, "S")
+        a_tp(1, 6)
+        mul(0, 2)
+        g_int(2, 2, "S")
+        dh_mm(1, 3, 7)
+        d_int(0, (0, 4), "V")
+        n_tp(0, 0, 0)
+        a_cp(1, "S")
+        g_int(2, 3, "S")
+        dh_mm(1, 1, 1)
+        x_tp(1, 0, 3)
+        a_quant()
+        g_int(2, 1, "S")
+        x_tp(1, 1, 4)
+        g_int(2, 0, "V")
+        n_cp(0, 0, "S")
+        dh_mm(1, 0, 2)
+        r_quant(0)
+        x_cp(1, 1, "S")
+        dx_mm(0, 1, 6)
+        x_cp(1, 0, "S")
+        mul(1, 1)
+        n_tp(0, 1, 0)
+        dx_cp(0, 1, "S")
+        mul(1, 0)
+        dx_mm(0, 3, 4)
+        mul(1, 3)
+        dx_mm(0, 2, 3)
+        g_int(3, 2, "S")
+        dx_mm(0, 0, 1)
+        mul(1, 2)
+        g_int(3, 3, "S")
+        g_quant(2)
+        dx_cp(0, 2, "S")
+        d_int(1, (0, 4), "V")
+        n_cp(0, 1, "S")
+        dh_mm(2, 1, 6)
+        n_tp(1, 1, 2)
+        g_int(3, 0, "S")
+        dh_mm(2, 2, 7)
+        mul(2, 1)
+        n_cp(1, 1, "S")
+        dh_mm(2, 0, 5)
+        n_tp(1, 0, 3)
+        r_quant(1)
+        g_int(3, 1, "S")
+        mul(2, 0)
+        dx_cp(0, 0, "S")
+        dx_mm(1, 1, 0)
+        dh_mm(2, 3, 6)
+        mul(2, 2)
+        n_cp(1, 0, "S")
+        x_tp(0, 0, 2)
+        g_quant(3)
+        dx_cp(0, 3, "S")
+        dx_mm(1, 2, 5)
+        mul(2, 3)
+        dx_cp(1, 1, "S")
+        dx_mm(1, 0, 1)
+        dx_store(0, 0, J)
+        n_tp(2, 0, 7)
+        x_quant(1)
+        dx_cp(1, 0, "S")
+        x_tp(2, 1, 3)
+        d_int(2, (0, 4), "V")
+        n_cp(2, 0, "S")
+        n_tp(2, 1, 4)
+        x_cp(0, 0, "S")
+        x_tp(2, 0, 6)
+        dx_cp(1, 2, "S")
+        dh_mm(3, 3, 0)
+        r_quant(2)
+        dx_mm(1, 3, 1)
+        n_cp(2, 1, "S")
+        dh_mm(3, 0, 7)
+        mul(3, 3)
+        dh_mm(3, 2, 2)
+        x_cp(2, 0, "S")
+        dx_mm(2, 3, 5)
+        mul(3, 0)
+        dh_mm(3, 1, 4)
+        x_cp(2, 1, "S")
+        dx_mm(2, 0, 0)
+        mul(3, 2)
+        dx_mm(2, 1, 6)
+        dx_cp(2, 3, "S")
+        x_tp(0, 1, 7)
+        mul(3, 1)
+        dx_cp(1, 3, "S")
+        x_tp(3, 0, 3)
+        n_quant(1)
+        x_cp(0, 1, "S")
+        x_tp(3, 1, 2)
+        dx_store(1, 0, J)
+        d_int(3, (0, 4), "V")
+        dx_cp(2, 0, "S")
+        da_mm(1, 3, 5)
+        dx_mm(2, 2, 4)
+        dx_cp(2, 1, "S")
+        n_tp(3, 0, 1)
+        dx_cp(2, 2, "S")
+        n_quant(0)
+        n_tp(3, 1, 7)
+        n_cp(3, 0, "S")
+        r_quant(3)
+        dx_store(2, 0, J)
+        da_mm(1, 1, 0)
+        n_cp(3, 1, "S")
+        x_quant(0)
+        dx_mm(3, 2, 6)
+        dx_mm(3, 3, 4)
+        n_quant(2)
+        dx_cp(3, 2, "S")
+        da_mm(0, 0, 1)
+        da_mm(0, 2, 7)
+        x_quant(2)
+        dx_cp(3, 3, "S")
+        dx_mm(3, 0, 6)
+        da_mm(0, 1)
+        x_cp(3, 0, "V")
+        x_cp(3, 1, "S")
+        da_mm(0, 3)
+        dx_store(3, 2, 4)
+        dx_mm(3, 1, 4)
+        n_quant(3)
+        dx_cp(3, 0, "S")
+        da_mm(2, 1)
+        da_mm(2, 3)
+        dx_cp(3, 1, "S")
+        x_quant(3)
+        da_mm(1, 2)
+        da_mm(1, 0)
+        dx_store(3, 0, 2)
+        da_mm(3, 3)
+        da_mm(3, 1)
+        da_cp(3, "S")
+        da_mm(2, 0)
+        da_mm(3, 2)
+        da_mm(2, 2)
+        da_cp(1, "S")
+        da_store(3)
+        da_mm(3, 0)
+        da_cp(2, "S")
+        da_store(1)
+        da_cp(0, "S")
+        da_store(2)
+        da_store(0)

@@ -21,6 +21,7 @@ U8 = mybir.dt.uint8
 E4 = mybir.dt.float8_e4m3fn_x4
 E5 = mybir.dt.float8_e5m2_x4
 MULT = mybir.AluOpType.mult
+X_SORTED = (2, 3)
 
 
 def tile_cptensorproduct_pa_v_kernel(tc, x1, A, t2, w, C, t3, grad_out, out_0, out_1):
@@ -45,7 +46,10 @@ def tile_cptensorproduct_pa_v_kernel(tc, x1, A, t2, w, C, t3, grad_out, out_0, o
             )
 
         g_raw = [raw("g_raw%d" % i, BF16) for i in range(G)]
-        x_raw = [keep.tile([P, J, B, CO], BF16, name="x_raw%d" % i, align_bytes=64) for i in range(G)]
+        x_raw = [
+            raw("x_raw%d" % i, BF16) if i in X_SORTED else keep.tile([P, J, B, CO], BF16, name="x_raw%d" % i, align_bytes=64)
+            for i in range(G)
+        ]
         t3_raw = [raw("t3_raw%d" % i, F32) for i in range(G)]
         c_raw = keep.tile([P, J, R], BF16, name="c_raw", align_bytes=64)
         a_raw = keep.tile([P, J, R], BF16, name="a_raw", align_bytes=64)
@@ -63,35 +67,29 @@ def tile_cptensorproduct_pa_v_kernel(tc, x1, A, t2, w, C, t3, grad_out, out_0, o
             )
 
         def load_x(i):
+            if i in X_SORTED:
+                load_group(x_raw[i], x1, i)
+                return
             for b in range(B):
                 nc.sync.dma_start(
                     out=x_raw[i][:, :, b, :], in_=x1[B * i + b].rearrange("(p j) c -> p j c", j=J)
                 )
 
-        c_view = C.rearrange("(p j) r -> p j r", j=J)
-        def load_c(h):
-            nc.sync.dma_start(out=c_raw[:, :, 256 * h : 256 * (h + 1)], in_=c_view[:, :, 256 * h : 256 * (h + 1)])
 
-        def load_t3_half(h):
-            view = t3[0:B].rearrange("b (p j) c -> p b j c", j=J)
-            nc.sync.dma_start(out=t3_raw[0][:, :, 2 * h : 2 * h + 2, :], in_=view[:, :, 2 * h : 2 * h + 2, :])
-
-        load_c(0)
-        load_c(1)
+        nc.sync.dma_start(out=c_raw[:], in_=C.rearrange("(p j) r -> p j r", j=J))
         load_pair(g_raw[0], grad_out, 0, 1)
-        load_group(g_raw[1], grad_out, 1)
-        load_pair(g_raw[0], grad_out, 0, 0)
-        nc.sync.dma_start(out=a_raw[:], in_=A.rearrange("(p j) r -> p j r", j=J))
-        load_t3_half(0)
-        load_t3_half(1)
         load_group(g_raw[2], grad_out, 2)
-        load_x(1)
-        load_group(t3_raw[1], t3, 1)
+        load_pair(g_raw[0], grad_out, 0, 0)
+        load_group(t3_raw[0], t3, 0)
+        load_group(g_raw[1], grad_out, 1)
+        nc.sync.dma_start(out=a_raw[:], in_=A.rearrange("(p j) r -> p j r", j=J))
         load_group(g_raw[3], grad_out, 3)
         load_group(t3_raw[2], t3, 2)
-        load_x(0)
         load_x(2)
+        load_group(t3_raw[1], t3, 1)
+        load_x(0)
         load_group(t3_raw[3], t3, 3)
+        load_x(1)
         load_x(3)
 
         ident = keep.tile([P, P], F32, name="ident")
@@ -135,25 +133,25 @@ def tile_cptensorproduct_pa_v_kernel(tc, x1, A, t2, w, C, t3, grad_out, out_0, o
 
         g_grp = {}
 
-        def g_int(i, b, eng):
+        def g_int(i, b0, b1, eng):
             if i not in g_grp:
                 g_grp[i] = ring.tile([P, NT, J], BF16, name="g_grp", align_bytes=64, bufs=3)
             tcopy(
                 eng,
-                g_grp[i][:, CO * b : CO * (b + 1), :].rearrange("p (c k) j -> p c j k", k=4),
-                g_raw[i][:, b].rearrange("p j (c k) -> p c j k", k=4),
+                g_grp[i][:, CO * b0 : CO * b1, :].rearrange("p (b c k) j -> p b c j k", b=b1 - b0, k=4),
+                g_raw[i][:, b0:b1].rearrange("p b j (c k) -> p b c j k", k=4),
+            )
+
+        def quantize_part(q, grouped, fmt, h):
+            words = slice(0, 512) if h is None else slice(256 * h, 256 * (h + 1))
+            nc.vector.quantize_mx(
+                out=q[0][:, words].bitcast(fmt),
+                scales=q[1][:, words],
+                in_=grouped[:, 4 * words.start : 4 * words.stop],
             )
 
         def g_quant(i, h=None):
-            flat = g_grp[i][:].rearrange("p n j -> p (n j)")
-            if h is None:
-                quantize(g_q[i], flat, E5)
-            else:
-                nc.vector.quantize_mx(
-                    out=g_q[i][0][:, 256 * h : 256 * (h + 1)].bitcast(E5),
-                    scales=g_q[i][1][:, 256 * h : 256 * (h + 1)],
-                    in_=flat[:, 1024 * h : 1024 * (h + 1)],
-                )
+            quantize_part(g_q[i], g_grp[i][:].rearrange("p n j -> p (n j)"), E5, h)
 
         dh = {}
 
@@ -185,8 +183,8 @@ def tile_cptensorproduct_pa_v_kernel(tc, x1, A, t2, w, C, t3, grad_out, out_0, o
                 dt1[i][:, :, cols].rearrange("p t (c k) -> p c t k", k=4),
             )
 
-        def r_quant(i):
-            quantize(r_q[i], d_int_tile[i][:].rearrange("p n t -> p (n t)"), E5)
+        def r_quant(i, h=None):
+            quantize_part(r_q[i], d_int_tile[i][:].rearrange("p n t -> p (n t)"), E5, h)
 
         def transposes(words, contiguous, h, tr):
             for s in range(2):
@@ -216,22 +214,33 @@ def tile_cptensorproduct_pa_v_kernel(tc, x1, A, t2, w, C, t3, grad_out, out_0, o
                 n_grp[i] = ring.tile([P, 2048], BF16, name="n_grp", align_bytes=64, bufs=4)
             tr_copy(eng, n_grp[i], h, n_tr[i, h])
 
-        def n_quant(i):
-            quantize(n_q[i], n_grp[i][:], E5)
+        def n_quant(i, h=None):
+            quantize_part(n_q[i], n_grp[i], E5, h)
 
-        x_tr, x_grp = {}, {}
+        x_w, x_tr, x_grp = {}, {}, {}
+
+        def x_pre(i, eng):
+            x_w[i] = ring.tile([P, 1024], F32, name="x_w", align_bytes=64)
+            tcopy(
+                eng,
+                x_w[i][:].rearrange("p (j u b q) -> p j u b q", j=J, u=2, b=B),
+                x_raw[i][:].rearrange("p b j c -> p (b j c)").bitcast(F32).rearrange("p (b j q u) -> p j u b q", b=B, j=J, u=2),
+            )
 
         def x_tp(i, h, k):
             x_tr[i, h] = bank(k)
-            transposes(x_raw[i][:].rearrange("p j b c -> p (j b c)").bitcast(F32), False, h, x_tr[i, h])
+            if i in X_SORTED:
+                transposes(x_w[i][:], True, h, x_tr[i, h])
+            else:
+                transposes(x_raw[i][:].rearrange("p j b c -> p (j b c)").bitcast(F32), False, h, x_tr[i, h])
 
         def x_cp(i, h, eng):
             if i not in x_grp:
                 x_grp[i] = ring.tile([P, 2048], BF16, name="x_grp", align_bytes=64, bufs=4)
             tr_copy(eng, x_grp[i], h, x_tr[i, h])
 
-        def x_quant(i):
-            quantize(x_q[i], x_grp[i][:], E4)
+        def x_quant(i, h=None):
+            quantize_part(x_q[i], x_grp[i], E4, h)
 
         a_tr = {}
         a_grp = keep.tile([P, 2048], BF16, name="a_grp", align_bytes=64)
@@ -285,173 +294,173 @@ def tile_cptensorproduct_pa_v_kernel(tc, x1, A, t2, w, C, t3, grad_out, out_0, o
         def da_store(j):
             nc.sync.dma_start(out=out_1.rearrange("(p j) r -> p j r", j=J)[:, j, :], in_=da_sb[:, j, :])
 
+        c_int(1, "V")
         c_int(0, "S")
-        g_int(0, 3, "V")
-        g_int(0, 2, "S")
-        c_int(1, "S")
-        g_quant(0, 1)
-        g_int(0, 0, "V")
-        g_int(0, 1, "S")
-        g_int(1, 3, "V")
-        g_int(1, 0, "S")
+        g_int(0, 3, 4, "V")
+        g_int(0, 2, 3, "S")
         quantize(c_q, c_grp[:], E4)
+        g_quant(0, 1)
+        g_int(2, 0, 3, "S")
+        g_int(2, 3, 4, "V")
+        g_int(0, 1, 2, "V")
+        g_int(0, 0, 1, "V")
         g_quant(0, 0)
-        g_int(1, 1, "S")
-        dh_mm(0, 0, 0)
-        g_int(1, 2, "S")
-        dh_mm(0, 3, 1)
-        mul(0, 0)
-        dh_mm(0, 2, 2)
-        g_quant(1)
-        dh_mm(0, 1, 3)
-        a_tp(0, 4)
-        mul(0, 3)
-        mul(0, 1)
-        dh_mm(1, 2, 5)
-        a_cp(0, "S")
-        a_tp(1, 6)
-        mul(0, 2)
-        g_int(2, 2, "S")
-        dh_mm(1, 3, 7)
-        d_int(0, (0, 4), "V")
-        n_tp(0, 0, 0)
-        a_cp(1, "S")
-        g_int(2, 3, "S")
-        dh_mm(1, 1, 1)
-        x_tp(1, 0, 3)
-        a_quant()
-        g_int(2, 1, "S")
-        x_tp(1, 1, 4)
-        g_int(2, 0, "V")
-        n_cp(0, 0, "S")
-        dh_mm(1, 0, 2)
-        r_quant(0)
-        x_cp(1, 1, "S")
-        dx_mm(0, 1, 6)
-        x_cp(1, 0, "S")
-        mul(1, 1)
-        n_tp(0, 1, 0)
-        dx_cp(0, 1, "S")
-        mul(1, 0)
-        dx_mm(0, 3, 4)
-        mul(1, 3)
-        dx_mm(0, 2, 3)
-        g_int(3, 2, "S")
-        dx_mm(0, 0, 1)
-        mul(1, 2)
-        g_int(3, 3, "S")
         g_quant(2)
-        dx_cp(0, 2, "S")
-        d_int(1, (0, 4), "V")
-        n_cp(0, 1, "S")
-        dh_mm(2, 1, 6)
-        n_tp(1, 1, 2)
-        g_int(3, 0, "S")
-        dh_mm(2, 2, 7)
-        mul(2, 1)
-        n_cp(1, 1, "S")
+        dh_mm(0, 2, 0)
+        dh_mm(0, 3, 1)
+        mul(0, 2)
+        dh_mm(0, 1, 2)
+        mul(0, 3)
+        dh_mm(2, 1, 3)
+        dh_mm(0, 0, 4)
+        mul(0, 1)
         dh_mm(2, 0, 5)
-        n_tp(1, 0, 3)
-        r_quant(1)
-        g_int(3, 1, "S")
-        mul(2, 0)
-        dx_cp(0, 0, "S")
-        dx_mm(1, 1, 0)
-        dh_mm(2, 3, 6)
-        mul(2, 2)
-        n_cp(1, 0, "S")
-        x_tp(0, 0, 2)
-        g_quant(3)
-        dx_cp(0, 3, "S")
-        dx_mm(1, 2, 5)
+        g_int(1, 0, 3, "S")
+        n_tp(0, 1, 6)
+        mul(0, 0)
+        dh_mm(2, 3, 7)
+        g_int(1, 3, 4, "V")
+        a_tp(1, 0)
+        d_int(0, (0, 4), "V")
+        n_cp(0, 1, "S")
+        a_tp(0, 1)
+        a_cp(1, "S")
+        n_tp(0, 0, 2)
+        g_quant(1)
+        dh_mm(2, 2, 4)
+        a_cp(0, "S")
+        g_int(3, 3, 4, "V")
+        dh_mm(1, 0, 6)
+        n_cp(0, 0, "S")
+        r_quant(0)
+        dh_mm(1, 1, 0)
+        g_int(3, 0, 3, "S")
+        a_quant()
         mul(2, 3)
-        dx_cp(1, 1, "S")
-        dx_mm(1, 0, 1)
-        dx_store(0, 0, J)
-        n_tp(2, 0, 7)
-        x_quant(1)
-        dx_cp(1, 0, "S")
-        x_tp(2, 1, 3)
+        dx_mm(0, 3, 1)
+        dx_mm(0, 0, 2)
+        mul(2, 2)
+        dx_mm(0, 1, 7)
+        dx_cp(0, 3, "S")
+        mul(2, 1)
+        dx_mm(0, 2, 4)
+        x_pre(2, "S")
+        mul(2, 0)
+        n_tp(2, 1, 1)
+        g_quant(3)
+        dh_mm(1, 2, 3)
+        dx_cp(0, 1, "S")
+        x_tp(2, 1, 5)
         d_int(2, (0, 4), "V")
-        n_cp(2, 0, "S")
-        n_tp(2, 1, 4)
-        x_cp(0, 0, "S")
-        x_tp(2, 0, 6)
-        dx_cp(1, 2, "S")
-        dh_mm(3, 3, 0)
-        r_quant(2)
-        dx_mm(1, 3, 1)
-        n_cp(2, 1, "S")
-        dh_mm(3, 0, 7)
-        mul(3, 3)
-        dh_mm(3, 2, 2)
-        x_cp(2, 0, "S")
-        dx_mm(2, 3, 5)
-        mul(3, 0)
-        dh_mm(3, 1, 4)
+        dx_cp(0, 0, "S")
+        dh_mm(3, 3, 7)
+        dx_cp(0, 2, "S")
+        dh_mm(1, 3, 2)
+        mul(1, 2)
         x_cp(2, 1, "S")
+        x_tp(2, 0, 4)
+        mul(1, 3)
+        n_cp(2, 1, "S")
+        n_tp(2, 0, 3)
+        dx_store(0, 0, J)
+        r_quant(2)
+        x_cp(2, 0, "S")
+        n_tp(1, 1, 5)
+        mul(1, 1)
+        dh_mm(3, 1, 2)
+        n_cp(2, 0, "S")
+        dx_mm(2, 2, 1)
+        mul(1, 0)
+        n_cp(1, 1, "S")
+        dx_mm(2, 1, 4)
         dx_mm(2, 0, 0)
-        mul(3, 2)
-        dx_mm(2, 1, 6)
-        dx_cp(2, 3, "S")
-        x_tp(0, 1, 7)
-        mul(3, 1)
-        dx_cp(1, 3, "S")
-        x_tp(3, 0, 3)
-        n_quant(1)
-        x_cp(0, 1, "S")
-        x_tp(3, 1, 2)
-        dx_store(1, 0, J)
-        d_int(3, (0, 4), "V")
-        dx_cp(2, 0, "S")
-        da_mm(1, 3, 5)
-        dx_mm(2, 2, 4)
-        dx_cp(2, 1, "S")
-        n_tp(3, 0, 1)
-        dx_cp(2, 2, "S")
         n_quant(0)
-        n_tp(3, 1, 7)
-        n_cp(3, 0, "S")
-        r_quant(3)
+        dx_cp(2, 2, "S")
+        dh_mm(3, 2, 3)
+        dx_mm(2, 3, 6)
+        d_int(1, (0, 4), "V")
+        n_tp(1, 0, 5)
+        dx_cp(2, 1, "S")
+        dx_cp(2, 0, "S")
+        x_tp(0, 0, 1)
+        x_tp(0, 1, 4)
+        dx_cp(2, 3, "S")
+        mul(3, 3)
+        dh_mm(3, 0, 0)
+        x_cp(0, 0, "S")
+        r_quant(1)
         dx_store(2, 0, J)
-        da_mm(1, 1, 0)
-        n_cp(3, 1, "S")
+        n_cp(1, 0, "S")
+        mul(3, 0)
+        dx_mm(1, 0, 6)
+        x_cp(0, 1, "S")
+        dx_mm(1, 3, 7)
+        mul(3, 1)
+        dx_mm(1, 1, 1)
+        x_tp(1, 1, 5)
+        dx_cp(1, 0, "S")
+        mul(3, 2)
+        dx_cp(1, 3, "S")
+        dx_mm(1, 2, 0)
         x_quant(0)
-        dx_mm(3, 2, 6)
-        dx_mm(3, 3, 4)
-        n_quant(2)
+        x_tp(1, 0, 4)
+        dx_cp(1, 1, "S")
+        d_int(3, (0, 2), "V")
+        da_mm(0, 0, 2)
+        dx_cp(1, 2, "S")
+        d_int(3, (2, 4), "V")
+        n_tp(3, 1, 6)
+        x_cp(1, 1, "S")
+        dx_store(1, 0, J)
+        n_tp(3, 0, 3)
+        r_quant(3, 0)
+        x_cp(1, 0, "S")
+        r_quant(3, 1)
+        da_mm(0, 3, 7)
+        x_pre(3, "V")
+        n_cp(3, 1, "S")
+        dx_mm(3, 1, 1)
+        dx_mm(3, 2, 0)
+        n_quant(1)
+        n_cp(3, 0, "S")
+        dx_mm(3, 3, 5)
+        da_mm(0, 2, 4)
+        x_quant(1)
         dx_cp(3, 2, "S")
-        da_mm(0, 0, 1)
-        da_mm(0, 2, 7)
-        x_quant(2)
+        x_tp(3, 1, 6)
+        x_tp(3, 0, 3)
         dx_cp(3, 3, "S")
-        dx_mm(3, 0, 6)
-        da_mm(0, 1)
-        x_cp(3, 0, "V")
-        x_cp(3, 1, "S")
-        da_mm(0, 3)
-        dx_store(3, 2, 4)
-        dx_mm(3, 1, 4)
-        n_quant(3)
-        dx_cp(3, 0, "S")
-        da_mm(2, 1)
-        da_mm(2, 3)
-        dx_cp(3, 1, "S")
-        x_quant(3)
-        da_mm(1, 2)
+        n_quant(3, 1)
         da_mm(1, 0)
-        dx_store(3, 0, 2)
-        da_mm(3, 3)
-        da_mm(3, 1)
-        da_cp(3, "S")
+        n_quant(2)
+        x_cp(3, 0, "S")
+        dx_mm(3, 0, 0)
+        dx_store(3, 2, 4)
+        da_mm(1, 1, 5)
+        x_quant(2)
+        dx_cp(3, 1, "S")
+        da_mm(1, 2)
+        da_mm(1, 3)
+        x_quant(3, 0)
+        dx_cp(3, 0, "S")
         da_mm(2, 0)
-        da_mm(3, 2)
-        da_mm(2, 2)
-        da_cp(1, "S")
-        da_store(3)
+        n_quant(3, 0)
+        da_mm(0, 1)
+        x_cp(3, 1, "S")
         da_mm(3, 0)
-        da_cp(2, "S")
-        da_store(1)
+        dx_store(3, 0, 2)
+        da_mm(3, 1)
         da_cp(0, "S")
-        da_store(2)
+        da_mm(2, 1)
+        x_quant(3, 1)
+        da_mm(2, 3)
+        da_cp(1, "S")
+        da_mm(3, 3)
         da_store(0)
+        da_mm(3, 2)
+        da_cp(3, "S")
+        da_mm(2, 2)
+        da_store(1)
+        da_cp(2, "V")
+        da_store(3)
+        da_store(2)

@@ -21,7 +21,7 @@ U8 = mybir.dt.uint8
 E4 = mybir.dt.float8_e4m3fn_x4
 E5 = mybir.dt.float8_e5m2_x4
 MULT = mybir.AluOpType.mult
-X_SORTED = (2, 3)
+X_SORTED = (1, 2, 3)
 
 
 def tile_cptensorproduct_pa_v_kernel(tc, x1, A, t2, w, C, t3, grad_out, out_0, out_1):
@@ -60,11 +60,8 @@ def tile_cptensorproduct_pa_v_kernel(tc, x1, A, t2, w, C, t3, grad_out, out_0, o
                 in_=src[B * i : B * (i + 1)].rearrange("b (p j) c -> p b (j c)", j=J),
             )
 
-        def load_pair(tile, src, i, h):
-            nc.sync.dma_start(
-                out=tile[:, 2 * h : 2 * h + 2].rearrange("p b j c -> p b (j c)"),
-                in_=src[B * i + 2 * h : B * i + 2 * h + 2].rearrange("b (p j) c -> p b (j c)", j=J),
-            )
+        def load_sample(tile, src, i, b):
+            nc.sync.dma_start(out=tile[:, b], in_=src[B * i + b].rearrange("(p j) c -> p j c", j=J))
 
         def load_x(i):
             if i in X_SORTED:
@@ -76,21 +73,23 @@ def tile_cptensorproduct_pa_v_kernel(tc, x1, A, t2, w, C, t3, grad_out, out_0, o
                 )
 
 
+        load_sample(g_raw[0], grad_out, 0, 2)
+        load_sample(g_raw[0], grad_out, 0, 3)
+        load_sample(g_raw[0], grad_out, 0, 0)
+        load_sample(g_raw[0], grad_out, 0, 1)
         nc.sync.dma_start(out=c_raw[:], in_=C.rearrange("(p j) r -> p j r", j=J))
-        load_pair(g_raw[0], grad_out, 0, 1)
         load_group(g_raw[2], grad_out, 2)
-        load_pair(g_raw[0], grad_out, 0, 0)
         load_group(t3_raw[0], t3, 0)
         load_group(g_raw[1], grad_out, 1)
         nc.sync.dma_start(out=a_raw[:], in_=A.rearrange("(p j) r -> p j r", j=J))
         load_group(g_raw[3], grad_out, 3)
         load_group(t3_raw[2], t3, 2)
+        load_x(1)
         load_x(2)
         load_group(t3_raw[1], t3, 1)
-        load_x(0)
-        load_group(t3_raw[3], t3, 3)
-        load_x(1)
         load_x(3)
+        load_group(t3_raw[3], t3, 3)
+        load_x(0)
 
         ident = keep.tile([P, P], F32, name="ident")
         make_identity(nc, ident[:])
@@ -294,173 +293,174 @@ def tile_cptensorproduct_pa_v_kernel(tc, x1, A, t2, w, C, t3, grad_out, out_0, o
         def da_store(j):
             nc.sync.dma_start(out=out_1.rearrange("(p j) r -> p j r", j=J)[:, j, :], in_=da_sb[:, j, :])
 
-        c_int(1, "V")
-        c_int(0, "S")
-        g_int(0, 3, 4, "V")
         g_int(0, 2, 3, "S")
-        quantize(c_q, c_grp[:], E4)
-        g_quant(0, 1)
-        g_int(2, 0, 3, "S")
-        g_int(2, 3, 4, "V")
+        g_int(0, 3, 4, "V")
         g_int(0, 1, 2, "V")
         g_int(0, 0, 1, "V")
         g_quant(0, 0)
-        g_quant(2)
-        dh_mm(0, 2, 0)
+        c_int(1, "S")
+        c_int(0, "V")
+        g_quant(0, 1)
+        g_int(2, 3, 4, "V")
+        g_int(2, 0, 3, "S")
+        quantize(c_q, c_grp[:], E4)
+        dh_mm(0, 0, 0)
         dh_mm(0, 3, 1)
-        mul(0, 2)
+        g_quant(2)
         dh_mm(0, 1, 2)
         mul(0, 3)
-        dh_mm(2, 1, 3)
-        dh_mm(0, 0, 4)
+        dh_mm(0, 2, 3)
         mul(0, 1)
-        dh_mm(2, 0, 5)
-        g_int(1, 0, 3, "S")
-        n_tp(0, 1, 6)
+        dh_mm(2, 0, 4)
+        dh_mm(2, 3, 5)
         mul(0, 0)
-        dh_mm(2, 3, 7)
+        dh_mm(2, 1, 6)
+        g_int(1, 0, 3, "S")
+        mul(0, 2)
+        n_tp(0, 0, 7)
         g_int(1, 3, 4, "V")
-        a_tp(1, 0)
+        a_tp(1, 1)
         d_int(0, (0, 4), "V")
-        n_cp(0, 1, "S")
-        a_tp(0, 1)
-        a_cp(1, "S")
-        n_tp(0, 0, 2)
-        g_quant(1)
-        dh_mm(2, 2, 4)
-        a_cp(0, "S")
-        g_int(3, 3, 4, "V")
-        dh_mm(1, 0, 6)
+        a_tp(0, 2)
         n_cp(0, 0, "S")
+        n_tp(0, 1, 0)
+        a_cp(1, "S")
+        g_quant(1)
+        a_cp(0, "S")
         r_quant(0)
-        dh_mm(1, 1, 0)
-        g_int(3, 0, 3, "S")
+        dh_mm(1, 1, 3)
+        n_cp(0, 1, "S")
         a_quant()
-        mul(2, 3)
-        dx_mm(0, 3, 1)
-        dx_mm(0, 0, 2)
-        mul(2, 2)
-        dx_mm(0, 1, 7)
-        dx_cp(0, 3, "S")
-        mul(2, 1)
-        dx_mm(0, 2, 4)
-        x_pre(2, "S")
-        mul(2, 0)
-        n_tp(2, 1, 1)
-        g_quant(3)
-        dh_mm(1, 2, 3)
-        dx_cp(0, 1, "S")
-        x_tp(2, 1, 5)
-        d_int(2, (0, 4), "V")
-        dx_cp(0, 0, "S")
-        dh_mm(3, 3, 7)
-        dx_cp(0, 2, "S")
-        dh_mm(1, 3, 2)
-        mul(1, 2)
-        x_cp(2, 1, "S")
-        x_tp(2, 0, 4)
-        mul(1, 3)
-        n_cp(2, 1, "S")
-        n_tp(2, 0, 3)
-        dx_store(0, 0, J)
-        r_quant(2)
-        x_cp(2, 0, "S")
-        n_tp(1, 1, 5)
-        mul(1, 1)
-        dh_mm(3, 1, 2)
-        n_cp(2, 0, "S")
-        dx_mm(2, 2, 1)
-        mul(1, 0)
-        n_cp(1, 1, "S")
-        dx_mm(2, 1, 4)
-        dx_mm(2, 0, 0)
+        g_int(3, 0, 3, "S")
         n_quant(0)
-        dx_cp(2, 2, "S")
-        dh_mm(3, 2, 3)
-        dx_mm(2, 3, 6)
-        d_int(1, (0, 4), "V")
-        n_tp(1, 0, 5)
-        dx_cp(2, 1, "S")
+        dx_mm(0, 2, 7)
+        mul(2, 1)
+        dh_mm(2, 2, 1)
+        dx_mm(0, 1, 2)
+        mul(2, 0)
+        dx_mm(0, 3, 0)
+        g_int(3, 3, 4, "S")
+        dx_mm(0, 0, 6)
+        mul(2, 2)
+        dh_mm(1, 3, 4)
+        dx_cp(0, 1, "S")
+        mul(2, 3)
+        n_tp(2, 0, 1)
+        dx_cp(0, 0, "S")
+        g_quant(3)
+        dh_mm(1, 2, 2)
+        dx_cp(0, 2, "S")
+        d_int(2, (0, 4), "V")
+        dh_mm(3, 0, 5)
+        dx_cp(0, 3, "S")
+        n_tp(2, 1, 6)
+        n_cp(2, 0, "S")
+        dx_store(0, 0, J)
+        dh_mm(1, 0, 7)
+        x_pre(1, "V")
+        x_pre(2, "S")
+        r_quant(2)
+        x_tp(1, 1, 0)
+        mul(1, 2)
+        n_cp(2, 1, "S")
+        dx_mm(2, 1, 1)
+        x_cp(1, 1, "S")
+        mul(1, 1)
+        dx_mm(2, 0, 6)
+        dx_mm(2, 3, 2)
+        mul(1, 3)
         dx_cp(2, 0, "S")
-        x_tp(0, 0, 1)
-        x_tp(0, 1, 4)
+        dx_mm(2, 2, 0)
+        x_tp(2, 0, 3)
+        mul(1, 0)
+        dx_cp(2, 1, "S")
+        dh_mm(3, 3, 4)
+        x_pre(3, "V")
         dx_cp(2, 3, "S")
-        mul(3, 3)
-        dh_mm(3, 0, 0)
-        x_cp(0, 0, "S")
-        r_quant(1)
+        n_tp(1, 0, 6)
+        d_int(1, (0, 4), "V")
+        dx_cp(2, 2, "S")
+        n_tp(1, 1, 7)
+        x_cp(2, 0, "S")
+        x_tp(1, 0, 1)
         dx_store(2, 0, J)
-        n_cp(1, 0, "S")
+        dh_mm(3, 1, 2)
+        n_cp(1, 1, "S")
         mul(3, 0)
-        dx_mm(1, 0, 6)
-        x_cp(0, 1, "S")
-        dx_mm(1, 3, 7)
+        dh_mm(3, 2, 0)
+        x_tp(3, 0, 3)
+        n_cp(1, 0, "S")
+        r_quant(1)
+        x_tp(2, 1, 7)
+        x_cp(3, 0, "S")
+        mul(3, 3)
+        dx_mm(1, 0, 5)
+        x_cp(2, 1, "S")
+        dx_mm(1, 1, 6)
         mul(3, 1)
-        dx_mm(1, 1, 1)
-        x_tp(1, 1, 5)
+        x_tp(0, 1, 3)
         dx_cp(1, 0, "S")
         mul(3, 2)
-        dx_cp(1, 3, "S")
-        dx_mm(1, 2, 0)
-        x_quant(0)
-        x_tp(1, 0, 4)
-        dx_cp(1, 1, "S")
+        x_tp(3, 1, 4)
+        x_cp(1, 0, "S")
+        x_quant(3, 0)
+        dx_mm(1, 2, 7)
         d_int(3, (0, 2), "V")
-        da_mm(0, 0, 2)
+        dx_cp(1, 1, "S")
+        dx_mm(1, 3, 2)
+        x_tp(0, 0, 5)
         dx_cp(1, 2, "S")
         d_int(3, (2, 4), "V")
-        n_tp(3, 1, 6)
-        x_cp(1, 1, "S")
-        dx_store(1, 0, J)
-        n_tp(3, 0, 3)
+        n_tp(3, 0, 0)
+        dx_cp(1, 3, "S")
         r_quant(3, 0)
-        x_cp(1, 0, "S")
+        n_tp(3, 1, 1)
         r_quant(3, 1)
-        da_mm(0, 3, 7)
-        x_pre(3, "V")
-        n_cp(3, 1, "S")
-        dx_mm(3, 1, 1)
-        dx_mm(3, 2, 0)
-        n_quant(1)
+        x_cp(0, 0, "S")
+        dx_store(1, 0, J)
+        x_quant(2)
+        dx_mm(3, 2, 6)
+        x_cp(0, 1, "S")
+        dx_mm(3, 0, 7)
+        n_quant(2)
+        dx_mm(3, 1, 2)
         n_cp(3, 0, "S")
-        dx_mm(3, 3, 5)
-        da_mm(0, 2, 4)
+        dx_cp(3, 0, "V")
+        da_mm(2, 2, 5)
+        dx_cp(3, 1, "S")
+        dx_mm(3, 3, 3)
+        x_quant(0)
+        da_mm(2, 0, 0)
+        n_cp(3, 1, "S")
+        da_mm(2, 3, 7)
+        dx_store(3, 0, 2)
         x_quant(1)
+        da_mm(2, 1, 2)
         dx_cp(3, 2, "S")
-        x_tp(3, 1, 6)
-        x_tp(3, 0, 3)
+        da_mm(0, 0)
+        n_quant(1)
+        da_mm(0, 1)
         dx_cp(3, 3, "S")
+        da_mm(0, 3)
         n_quant(3, 1)
         da_mm(1, 0)
-        n_quant(2)
-        x_cp(3, 0, "S")
-        dx_mm(3, 0, 0)
-        dx_store(3, 2, 4)
-        da_mm(1, 1, 5)
-        x_quant(2)
-        dx_cp(3, 1, "S")
-        da_mm(1, 2)
-        da_mm(1, 3)
-        x_quant(3, 0)
-        dx_cp(3, 0, "S")
-        da_mm(2, 0)
-        n_quant(3, 0)
-        da_mm(0, 1)
         x_cp(3, 1, "S")
-        da_mm(3, 0)
-        dx_store(3, 0, 2)
+        n_quant(3, 0)
+        dx_store(3, 2, 4)
+        da_mm(1, 1)
         da_mm(3, 1)
-        da_cp(0, "S")
-        da_mm(2, 1)
         x_quant(3, 1)
-        da_mm(2, 3)
+        da_mm(1, 3)
         da_cp(1, "S")
+        da_mm(3, 0)
         da_mm(3, 3)
-        da_store(0)
-        da_mm(3, 2)
-        da_cp(3, "S")
-        da_mm(2, 2)
+        da_mm(1, 2)
+        da_cp(0, "S")
         da_store(1)
-        da_cp(2, "V")
+        da_cp(3, "V")
+        da_mm(3, 2)
+        da_mm(0, 2)
+        da_store(0)
         da_store(3)
+        da_cp(2, "S")
         da_store(2)

@@ -3,25 +3,29 @@ from contextlib import ExitStack
 import concourse.mybir as mybir
 from concourse.masks import make_identity
 
-NB, D, CO, R = 16, 512, 128, 512
-N = NB * CO
-FLOPS = 3 * 2 * D * R * N
-BYTES = 2 * (2 * NB * D * CO + 2 * D * R) + 4 * (2 * NB * D * CO + D * R)
+SAMPLES, D, CO, R = 16, 512, 128, 512
+TOKENS = SAMPLES * CO
+FLOPS = 3 * 2 * D * R * TOKENS
+BYTES = 2 * (2 * D * TOKENS + 2 * D * R) + 4 * (R * TOKENS + D * TOKENS + D * R)
 
 P = 128
 J = 4
-G = 4
 B = 4
+G = SAMPLES // B
 NT = B * CO
+BANKS = 8
+BANK = 512
+
+X_SORTED_ON_ENGINE = (2, 3)
 
 F32 = mybir.dt.float32
 BF16 = mybir.dt.bfloat16
 U32 = mybir.dt.uint32
 U8 = mybir.dt.uint8
-E4 = mybir.dt.float8_e4m3fn_x4
-E5 = mybir.dt.float8_e5m2_x4
-MULT = mybir.AluOpType.mult
-X_SORTED = (1, 2, 3)
+E4M3 = mybir.dt.float8_e4m3fn_x4
+E5M2 = mybir.dt.float8_e5m2_x4
+
+VECTOR, SCALAR = "vector", "scalar"
 
 
 def tile_cptensorproduct_pa_v_kernel(tc, x1, A, t2, w, C, t3, grad_out, out_0, out_1):
@@ -29,438 +33,469 @@ def tile_cptensorproduct_pa_v_kernel(tc, x1, A, t2, w, C, t3, grad_out, out_0, o
     with ExitStack() as ctx:
         keep = ctx.enter_context(tc.tile_pool(name="keep", bufs=1))
         ring = ctx.enter_context(tc.tile_pool(name="ring", bufs=2))
-        outs = ctx.enter_context(tc.tile_pool(name="outs", bufs=4))
         psum = ctx.enter_context(tc.psum_pool(name="psum", bufs=1))
         ctx.enter_context(tc.manual_schedule())
 
-        def bank(k):
-            return psum.tile([P, 512], F32, name="bank%d" % k, tag="bank%d" % k)
 
-        def raw(name, dtype):
+        def by_sample(name, dtype):
             return keep.tile([P, B, J, CO], dtype, name=name, align_bytes=64)
 
-        def codes(name):
+        g_raw = [by_sample("g_raw%d" % i, BF16) for i in range(G)]
+        t3_raw = [by_sample("t3_raw%d" % i, F32) for i in range(G)]
+        x_raw = [
+            by_sample("x_raw%d" % i, BF16)
+            if i in X_SORTED_ON_ENGINE
+            else keep.tile([P, J, B, CO], BF16, name="x_raw%d" % i, align_bytes=64)
+            for i in range(G)
+        ]
+        c_raw = keep.tile([P, J, R], BF16, name="c_raw", align_bytes=64)
+        a_raw = keep.tile([P, J, R], BF16, name="a_raw", align_bytes=64)
+
+        def load_matrix(tile, matrix):
+            nc.sync.dma_start(out=tile[:], in_=matrix.rearrange("(p j) r -> p j r", j=J))
+
+        def load_samples(tile, tensor, i, b0, b1):
+            nc.sync.dma_start(
+                out=tile[:, b0:b1].rearrange("p b j c -> p b (j c)"),
+                in_=tensor[B * i + b0 : B * i + b1].rearrange("b (p j) c -> p b (j c)", j=J),
+            )
+
+        def load_t3_half(h):
+            rows = slice(2 * h, 2 * h + 2)
+            view = t3[0:B].rearrange("b (p j) c -> p b j c", j=J)
+            nc.sync.dma_start(out=t3_raw[0][:, :, rows, :], in_=view[:, :, rows, :])
+
+        def load_x(i):
+            if i in X_SORTED_ON_ENGINE:
+                load_samples(x_raw[i], x1, i, 0, B)
+            else:
+                for b in range(B):
+                    nc.sync.dma_start(
+                        out=x_raw[i][:, :, b, :], in_=x1[B * i + b].rearrange("(p j) c -> p j c", j=J)
+                    )
+
+        load_matrix(c_raw, C)
+        load_samples(g_raw[0], grad_out, 0, 3, 4)
+        load_samples(g_raw[0], grad_out, 0, 2, 3)
+        load_samples(g_raw[2], grad_out, 2, 0, B)
+        load_samples(g_raw[0], grad_out, 0, 1, 2)
+        load_samples(g_raw[0], grad_out, 0, 0, 1)
+        load_samples(g_raw[1], grad_out, 1, 0, B)
+        load_t3_half(1)
+        load_t3_half(0)
+        load_matrix(a_raw, A)
+        load_samples(g_raw[3], grad_out, 3, 0, B)
+        load_samples(t3_raw[2], t3, 2, 0, B)
+        load_x(2)
+        load_samples(t3_raw[1], t3, 1, 0, B)
+        load_x(0)
+        load_samples(t3_raw[3], t3, 3, 0, B)
+        load_x(1)
+        load_x(3)
+
+        identity = keep.tile([P, P], F32, name="identity")
+        make_identity(nc, identity[:])
+
+
+        empty = list(range(BANKS))
+
+        def open_bank():
+            k = empty[0]
+            empty.remove(k)
+            return k, psum.tile([P, BANK], F32, name="bank%d" % k)
+
+        def copy(engine, out, in_):
+            if engine == VECTOR:
+                nc.vector.tensor_copy(out=out, in_=in_)
+            else:
+                nc.scalar.copy(out=out, in_=in_)
+
+        def copy_from_bank(engine, out, bank, in_):
+            copy(engine, out, in_)
+            empty.append(bank[0])
+
+        def operand(name):
             return (
                 keep.tile([P, 512], U32, name=name + "_codes", align_bytes=64),
                 keep.tile([P, 512], U8, name=name + "_scales", align_bytes=64),
             )
 
-        g_raw = [raw("g_raw%d" % i, BF16) for i in range(G)]
-        x_raw = [
-            raw("x_raw%d" % i, BF16) if i in X_SORTED else keep.tile([P, J, B, CO], BF16, name="x_raw%d" % i, align_bytes=64)
-            for i in range(G)
-        ]
-        t3_raw = [raw("t3_raw%d" % i, F32) for i in range(G)]
-        c_raw = keep.tile([P, J, R], BF16, name="c_raw", align_bytes=64)
-        a_raw = keep.tile([P, J, R], BF16, name="a_raw", align_bytes=64)
-
-        def load_group(tile, src, i):
-            nc.sync.dma_start(
-                out=tile[:].rearrange("p b j c -> p b (j c)"),
-                in_=src[B * i : B * (i + 1)].rearrange("b (p j) c -> p b (j c)", j=J),
+        def quantize(op, grouped, fmt, half=None):
+            n0, n1 = (0, 512) if half is None else (256 * half, 256 * (half + 1))
+            nc.vector.quantize_mx(
+                out=op[0][:, n0:n1].bitcast(fmt), scales=op[1][:, n0:n1], in_=grouped[:, J * n0 : J * n1]
             )
 
-        def load_sample(tile, src, i, b):
-            nc.sync.dma_start(out=tile[:, b], in_=src[B * i + b].rearrange("(p j) c -> p j c", j=J))
-
-        def load_x(i):
-            if i in X_SORTED:
-                load_group(x_raw[i], x1, i)
-                return
-            for b in range(B):
-                nc.sync.dma_start(
-                    out=x_raw[i][:, :, b, :], in_=x1[B * i + b].rearrange("(p j) c -> p j c", j=J)
-                )
-
-
-        load_sample(g_raw[0], grad_out, 0, 2)
-        load_sample(g_raw[0], grad_out, 0, 3)
-        load_sample(g_raw[0], grad_out, 0, 0)
-        load_sample(g_raw[0], grad_out, 0, 1)
-        nc.sync.dma_start(out=c_raw[:], in_=C.rearrange("(p j) r -> p j r", j=J))
-        load_group(g_raw[2], grad_out, 2)
-        load_group(t3_raw[0], t3, 0)
-        load_group(g_raw[1], grad_out, 1)
-        nc.sync.dma_start(out=a_raw[:], in_=A.rearrange("(p j) r -> p j r", j=J))
-        load_group(g_raw[3], grad_out, 3)
-        load_group(t3_raw[2], t3, 2)
-        load_x(1)
-        load_x(2)
-        load_group(t3_raw[1], t3, 1)
-        load_x(3)
-        load_group(t3_raw[3], t3, 3)
-        load_x(0)
-
-        ident = keep.tile([P, P], F32, name="ident")
-        make_identity(nc, ident[:])
-
-        c_q = codes("c")
-        a_q = codes("a")
-        g_q = [codes("g%d" % i) for i in range(G)]
-        x_q = [codes("x%d" % i) for i in range(G)]
-        r_q = [codes("r%d" % i) for i in range(G)]
-        n_q = [codes("n%d" % i) for i in range(G)]
-
-        def quantize(q, grouped, fmt):
-            nc.vector.quantize_mx(out=q[0][:].bitcast(fmt), scales=q[1][:], in_=grouped)
-
-        def mm(out, lhs, col, lfmt, rhs, rfmt, start, stop):
+        def multiply_mx(out, stationary, column_tile, stationary_fmt, moving, moving_fmt, start, stop):
+            cols = slice(P * column_tile, P * (column_tile + 1))
             nc.tensor.matmul_mx(
                 out=out[:],
-                lhsT=lhs[0][:, P * col : P * (col + 1)].bitcast(lfmt),
-                lhsT_scale=lhs[1][:, P * col : P * (col + 1)],
-                rhs=rhs[0][:].bitcast(rfmt),
-                rhs_scale=rhs[1][:],
+                lhsT=stationary[0][:, cols].bitcast(stationary_fmt),
+                lhsT_scale=stationary[1][:, cols],
+                rhs=moving[0][:].bitcast(moving_fmt),
+                rhs_scale=moving[1][:],
                 start=start,
                 stop=stop,
             )
 
-        def tcopy(eng, out, in_):
-            if eng == "S":
-                nc.scalar.copy(out=out, in_=in_)
-            else:
-                nc.vector.tensor_copy(out=out, in_=in_)
+        def transpose_words(words, word_step, half, bank):
+            for s in range(2):
+                for u in range(2):
+                    first = 256 * (2 * half + s) + (u if word_step == 2 else P * u)
+                    block = words[:, first : first + word_step * (P - 1) + 1 : word_step]
+                    nc.tensor.transpose(bank[1][:, P * (2 * s + u) : P * (2 * s + u + 1)], block, identity[:])
 
-        c_grp = keep.tile([P, R * J], BF16, name="c_grp", align_bytes=64)
-
-        def c_int(h, eng):
-            tcopy(
-                eng,
-                c_grp[:].rearrange("p (t m j) -> p t m j", t=J, j=J)[:, :, 64 * h : 64 * (h + 1), :],
-                c_raw[:, :, 256 * h : 256 * (h + 1)].rearrange("p j (m t) -> p t m j", t=J),
+        def copy_words(engine, grouped, half, bank):
+            copy_from_bank(
+                engine,
+                grouped[:].bitcast(F32)[:, BANK * half : BANK * (half + 1)].rearrange("p (s k u) -> p s k u", s=2, u=2),
+                bank,
+                bank[1][:].rearrange("p (s u k) -> p s k u", s=2, u=2),
             )
 
-        g_grp = {}
 
-        def g_int(i, b0, b1, eng):
-            if i not in g_grp:
-                g_grp[i] = ring.tile([P, NT, J], BF16, name="g_grp", align_bytes=64, bufs=3)
-            tcopy(
-                eng,
-                g_grp[i][:, CO * b0 : CO * b1, :].rearrange("p (b c k) j -> p b c j k", b=b1 - b0, k=4),
+        c_op = operand("c")
+        c_grouped = keep.tile([P, R * J], BF16, name="c_grouped", align_bytes=64)
+
+        def c_interleave(half, engine):
+            copy(
+                engine,
+                c_grouped[:].rearrange("p (t m j) -> p t m j", t=J, j=J)[:, :, 64 * half : 64 * (half + 1), :],
+                c_raw[:, :, 256 * half : 256 * (half + 1)].rearrange("p j (m t) -> p t m j", t=J),
+            )
+
+        def c_quantize():
+            quantize(c_op, c_grouped, E4M3)
+
+        g_op = [operand("g%d" % i) for i in range(G)]
+        g_grouped = {}
+
+        def g_interleave(i, b0, b1, engine):
+            if i not in g_grouped:
+                g_grouped[i] = ring.tile([P, NT, J], BF16, name="g_grouped", align_bytes=64, bufs=3)
+            copy(
+                engine,
+                g_grouped[i][:, CO * b0 : CO * b1, :].rearrange("p (b c k) j -> p b c j k", b=b1 - b0, k=4),
                 g_raw[i][:, b0:b1].rearrange("p b j (c k) -> p b c j k", k=4),
             )
 
-        def quantize_part(q, grouped, fmt, h):
-            words = slice(0, 512) if h is None else slice(256 * h, 256 * (h + 1))
-            nc.vector.quantize_mx(
-                out=q[0][:, words].bitcast(fmt),
-                scales=q[1][:, words],
-                in_=grouped[:, 4 * words.start : 4 * words.stop],
-            )
+        def g_quantize(i, half=None):
+            quantize(g_op[i], g_grouped[i][:].rearrange("p n j -> p (n j)"), E5M2, half)
 
-        def g_quant(i, h=None):
-            quantize_part(g_q[i], g_grp[i][:].rearrange("p n j -> p (n j)"), E5, h)
 
         dh = {}
-
-        def dh_mm(i, t, k):
-            dh[i, t] = bank(k)
-            mm(dh[i, t], c_q, t, E4, g_q[i], E5, True, True)
-
         dt1 = {}
 
-        def mul(i, t):
+        def dh_matmul(i, t):
+            dh[i, t] = open_bank()
+            multiply_mx(dh[i, t][1], c_op, t, E4M3, g_op[i], E5M2, True, True)
+
+        def multiply(i, t):
             if i not in dt1:
                 dt1[i] = ring.tile([P, J, NT], BF16, name="dt1", align_bytes=64)
             nc.vector.tensor_tensor(
                 out=dt1[i][:, t, :].rearrange("p (b c) -> p b c", b=B),
-                in0=dh[i, t][:].rearrange("p (b c) -> p b c", b=B),
+                in0=dh[i, t][1][:].rearrange("p (b c) -> p b c", b=B),
                 in1=t3_raw[i][:, :, t, :],
-                op=MULT,
+                op=mybir.AluOpType.mult,
+            )
+            empty.append(dh[i, t][0])
+
+        r_op = [operand("r%d" % i) for i in range(G)]
+        r_grouped = {}
+
+        def r_interleave(i, engine, half=None):
+            if i not in r_grouped:
+                r_grouped[i] = ring.tile([P, NT, J], BF16, name="r_grouped", align_bytes=64)
+            n0, n1 = (0, NT) if half is None else (256 * half, 256 * (half + 1))
+            copy(
+                engine,
+                r_grouped[i][:, n0:n1, :].rearrange("p (c k) t -> p c t k", k=4),
+                dt1[i][:, :, n0:n1].rearrange("p t (c k) -> p c t k", k=4),
             )
 
-        d_int_tile = {}
+        def r_quantize(i, half=None):
+            quantize(r_op[i], r_grouped[i][:].rearrange("p n t -> p (n t)"), E5M2, half)
 
-        def d_int(i, q, eng):
-            if i not in d_int_tile:
-                d_int_tile[i] = ring.tile([P, NT, J], BF16, name="dt1_grp", align_bytes=64)
-            cols = slice(CO * q[0], CO * q[1])
-            tcopy(
-                eng,
-                d_int_tile[i][:, cols, :].rearrange("p (c k) t -> p c t k", k=4),
-                dt1[i][:, :, cols].rearrange("p t (c k) -> p c t k", k=4),
+        n_op = [operand("n%d" % i) for i in range(G)]
+        n_bank = {}
+        n_grouped = {}
+
+        def n_transpose(i, half):
+            n_bank[i, half] = open_bank()
+            transpose_words(dt1[i][:].rearrange("p t n -> p (t n)").bitcast(F32), 2, half, n_bank[i, half])
+
+        def n_copy(i, half, engine):
+            if i not in n_grouped:
+                n_grouped[i] = keep.tile([P, J * R], BF16, name="n_grouped%d" % i, align_bytes=64)
+            copy_words(engine, n_grouped[i], half, n_bank[i, half])
+
+        def n_quantize(i, half=None):
+            quantize(n_op[i], n_grouped[i], E5M2, half)
+
+
+        x_op = [operand("x%d" % i) for i in range(G)]
+        x_sorted = {}
+        x_bank = {}
+        x_grouped = {}
+
+        def x_sort(i, engine):
+            x_sorted[i] = ring.tile([P, J * NT // 2], F32, name="x_sorted", align_bytes=64)
+            words = x_raw[i][:].rearrange("p b j c -> p (b j c)").bitcast(F32)
+            copy(
+                engine,
+                x_sorted[i][:].rearrange("p (j u b q) -> p j u b q", j=J, u=2, b=B),
+                words.rearrange("p (b j q u) -> p j u b q", b=B, j=J, u=2),
             )
 
-        def r_quant(i, h=None):
-            quantize_part(r_q[i], d_int_tile[i][:].rearrange("p n t -> p (n t)"), E5, h)
-
-        def transposes(words, contiguous, h, tr):
-            for s in range(2):
-                for u in range(2):
-                    base = 256 * (2 * h + s)
-                    if contiguous:
-                        src = words[:, base + P * u : base + P * (u + 1)]
-                    else:
-                        src = words[:, base + u : base + 256 : 2]
-                    nc.tensor.transpose(tr[:, 256 * s + P * u : 256 * s + P * (u + 1)], src, ident[:])
-
-        def tr_copy(eng, grouped, h, tr):
-            tcopy(
-                eng,
-                grouped[:].bitcast(F32)[:, 512 * h : 512 * (h + 1)].rearrange("p (s k u) -> p s k u", s=2, u=2),
-                tr[:].rearrange("p (s u k) -> p s k u", s=2, u=2),
-            )
-
-        n_tr, n_grp = {}, {}
-
-        def n_tp(i, h, k):
-            n_tr[i, h] = bank(k)
-            transposes(dt1[i][:].rearrange("p t n -> p (t n)").bitcast(F32), False, h, n_tr[i, h])
-
-        def n_cp(i, h, eng):
-            if i not in n_grp:
-                n_grp[i] = ring.tile([P, 2048], BF16, name="n_grp", align_bytes=64, bufs=4)
-            tr_copy(eng, n_grp[i], h, n_tr[i, h])
-
-        def n_quant(i, h=None):
-            quantize_part(n_q[i], n_grp[i], E5, h)
-
-        x_w, x_tr, x_grp = {}, {}, {}
-
-        def x_pre(i, eng):
-            x_w[i] = ring.tile([P, 1024], F32, name="x_w", align_bytes=64)
-            tcopy(
-                eng,
-                x_w[i][:].rearrange("p (j u b q) -> p j u b q", j=J, u=2, b=B),
-                x_raw[i][:].rearrange("p b j c -> p (b j c)").bitcast(F32).rearrange("p (b j q u) -> p j u b q", b=B, j=J, u=2),
-            )
-
-        def x_tp(i, h, k):
-            x_tr[i, h] = bank(k)
-            if i in X_SORTED:
-                transposes(x_w[i][:], True, h, x_tr[i, h])
+        def x_transpose(i, half):
+            x_bank[i, half] = open_bank()
+            if i in X_SORTED_ON_ENGINE:
+                transpose_words(x_sorted[i], 1, half, x_bank[i, half])
             else:
-                transposes(x_raw[i][:].rearrange("p j b c -> p (j b c)").bitcast(F32), False, h, x_tr[i, h])
+                transpose_words(x_raw[i][:].rearrange("p j b c -> p (j b c)").bitcast(F32), 2, half, x_bank[i, half])
 
-        def x_cp(i, h, eng):
-            if i not in x_grp:
-                x_grp[i] = ring.tile([P, 2048], BF16, name="x_grp", align_bytes=64, bufs=4)
-            tr_copy(eng, x_grp[i], h, x_tr[i, h])
+        def x_copy(i, half, engine):
+            if i not in x_grouped:
+                x_grouped[i] = keep.tile([P, J * D], BF16, name="x_grouped%d" % i, align_bytes=64)
+            copy_words(engine, x_grouped[i], half, x_bank[i, half])
 
-        def x_quant(i, h=None):
-            quantize_part(x_q[i], x_grp[i], E4, h)
+        def x_quantize(i, half=None):
+            quantize(x_op[i], x_grouped[i], E4M3, half)
 
-        a_tr = {}
-        a_grp = keep.tile([P, 2048], BF16, name="a_grp", align_bytes=64)
 
-        def a_tp(h, k):
-            a_tr[h] = bank(k)
-            transposes(a_raw[:].rearrange("p j r -> p (j r)").bitcast(F32), False, h, a_tr[h])
+        a_op = operand("a")
+        a_bank = {}
+        a_grouped = keep.tile([P, J * D], BF16, name="a_grouped", align_bytes=64)
 
-        def a_cp(h, eng):
-            tr_copy(eng, a_grp, h, a_tr[h])
+        def a_transpose(half):
+            a_bank[half] = open_bank()
+            transpose_words(a_raw[:].rearrange("p j r -> p (j r)").bitcast(F32), 2, half, a_bank[half])
 
-        def a_quant():
-            quantize(a_q, a_grp[:], E4)
+        def a_copy(half, engine):
+            copy_words(engine, a_grouped, half, a_bank[half])
 
-        dx, dx_sb = {}, {}
+        def a_quantize():
+            quantize(a_op, a_grouped, E4M3)
 
-        def dx_mm(i, j, k):
-            dx[i, j] = bank(k)
-            mm(dx[i, j], a_q, j, E4, r_q[i], E5, True, True)
 
-        def dx_cp(i, j, eng):
-            if i not in dx_sb:
-                dx_sb[i] = outs.tile([P, B, J, CO], F32, name="dx_sb", align_bytes=64)
-            tcopy(eng, dx_sb[i][:, :, j, :], dx[i, j][:].rearrange("p (b c) -> p b c", b=B))
+        dx = {}
+        dx_rows = {}
+
+        def dx_matmul(i, j):
+            dx[i, j] = open_bank()
+            multiply_mx(dx[i, j][1], a_op, j, E4M3, r_op[i], E5M2, True, True)
+
+        def dx_copy(i, j, engine):
+            if i not in dx_rows:
+                dx_rows[i] = ring.tile([P, B, J, CO], F32, name="dx_rows", align_bytes=64, bufs=3)
+            copy_from_bank(engine, dx_rows[i][:, :, j, :], dx[i, j], dx[i, j][1][:].rearrange("p (b c) -> p b c", b=B))
 
         def dx_store(i, j0, j1):
             nc.sync.dma_start(
-                out=out_0[B * i : B * (i + 1)].rearrange("b (p j) c -> p b j c", j=J)[:, :, j0:j1, :].rearrange("p b j c -> p b (j c)") if j1 - j0 == J else out_0[B * i : B * (i + 1)].rearrange("b (p j) c -> p b j c", j=J)[:, :, j0:j1, :],
-                in_=dx_sb[i][:].rearrange("p b j c -> p b (j c)") if j1 - j0 == J else dx_sb[i][:, :, j0:j1, :],
+                out=out_0[B * i : B * (i + 1)].rearrange("b (p j) c -> p b j c", j=J)[:, :, j0:j1, :],
+                in_=dx_rows[i][:, :, j0:j1, :],
             )
+
 
         da = {}
-        da_sb = keep.tile([P, J, R], F32, name="da_sb", align_bytes=64)
+        da_passes = {}
+        da_rows = keep.tile([P, J, R], F32, name="da_rows", align_bytes=64)
+        da_view = out_1.rearrange("(p j) r -> p j r", j=J)
 
-        da_done = {}
-
-        def da_mm(i, j, k=None):
+        def da_matmul(i, j):
             if j not in da:
-                da[j] = bank(k)
-                da_done[j] = 0
-            mm(da[j], x_q[i], j, E4, n_q[i], E5, da_done[j] == 0, da_done[j] == G - 1)
-            da_done[j] += 1
+                da[j] = open_bank()
+                da_passes[j] = 0
+            da_passes[j] += 1
+            multiply_mx(da[j][1], x_op[i], j, E4M3, n_op[i], E5M2, da_passes[j] == 1, da_passes[j] == G)
 
-        def da_cp(j, eng):
-            tcopy(
-                eng,
-                da_sb[:, j, :].rearrange("p (m t) -> p m t", t=J),
-                da[j][:].rearrange("p (t m) -> p m t", t=J),
+        def da_copy(j, half, engine):
+            copy(
+                engine,
+                da_rows[:, j, 256 * half : 256 * (half + 1)].rearrange("p (m t) -> p m t", t=J),
+                da[j][1][:].rearrange("p (t m) -> p m t", t=J)[:, 64 * half : 64 * (half + 1), :],
             )
 
-        def da_store(j):
-            nc.sync.dma_start(out=out_1.rearrange("(p j) r -> p j r", j=J)[:, j, :], in_=da_sb[:, j, :])
+        def da_store(j, half):
+            cols = slice(256 * half, 256 * (half + 1))
+            nc.sync.dma_start(out=da_view[:, j, cols], in_=da_rows[:, j, cols])
 
-        g_int(0, 2, 3, "S")
-        g_int(0, 3, 4, "V")
-        g_int(0, 1, 2, "V")
-        g_int(0, 0, 1, "V")
-        g_quant(0, 0)
-        c_int(1, "S")
-        c_int(0, "V")
-        g_quant(0, 1)
-        g_int(2, 3, 4, "V")
-        g_int(2, 0, 3, "S")
-        quantize(c_q, c_grp[:], E4)
-        dh_mm(0, 0, 0)
-        dh_mm(0, 3, 1)
-        g_quant(2)
-        dh_mm(0, 1, 2)
-        mul(0, 3)
-        dh_mm(0, 2, 3)
-        mul(0, 1)
-        dh_mm(2, 0, 4)
-        dh_mm(2, 3, 5)
-        mul(0, 0)
-        dh_mm(2, 1, 6)
-        g_int(1, 0, 3, "S")
-        mul(0, 2)
-        n_tp(0, 0, 7)
-        g_int(1, 3, 4, "V")
-        a_tp(1, 1)
-        d_int(0, (0, 4), "V")
-        a_tp(0, 2)
-        n_cp(0, 0, "S")
-        n_tp(0, 1, 0)
-        a_cp(1, "S")
-        g_quant(1)
-        a_cp(0, "S")
-        r_quant(0)
-        dh_mm(1, 1, 3)
-        n_cp(0, 1, "S")
-        a_quant()
-        g_int(3, 0, 3, "S")
-        n_quant(0)
-        dx_mm(0, 2, 7)
-        mul(2, 1)
-        dh_mm(2, 2, 1)
-        dx_mm(0, 1, 2)
-        mul(2, 0)
-        dx_mm(0, 3, 0)
-        g_int(3, 3, 4, "S")
-        dx_mm(0, 0, 6)
-        mul(2, 2)
-        dh_mm(1, 3, 4)
-        dx_cp(0, 1, "S")
-        mul(2, 3)
-        n_tp(2, 0, 1)
-        dx_cp(0, 0, "S")
-        g_quant(3)
-        dh_mm(1, 2, 2)
-        dx_cp(0, 2, "S")
-        d_int(2, (0, 4), "V")
-        dh_mm(3, 0, 5)
-        dx_cp(0, 3, "S")
-        n_tp(2, 1, 6)
-        n_cp(2, 0, "S")
+        c_interleave(0, VECTOR)
+        c_interleave(1, SCALAR)
+        g_interleave(0, 2, 3, VECTOR)
+        g_interleave(0, 3, 4, VECTOR)
+        c_quantize()
+        g_interleave(2, 0, 3, SCALAR)
+        g_interleave(0, 1, 2, VECTOR)
+        g_interleave(0, 0, 1, VECTOR)
+        g_quantize(0, 1)
+        g_quantize(0, 0)
+        g_interleave(2, 3, 4, VECTOR)
+        dh_matmul(0, 2)
+        g_interleave(1, 0, 3, SCALAR)
+        g_quantize(2)
+        dh_matmul(0, 3)
+        multiply(0, 2)
+        dh_matmul(0, 1)
+        multiply(0, 3)
+        dh_matmul(0, 0)
+        g_interleave(1, 3, 4, SCALAR)
+        multiply(0, 1)
+        n_transpose(0, 1)
+        multiply(0, 0)
+        n_copy(0, 1, SCALAR)
+        a_transpose(1)
+        g_quantize(1)
+        a_transpose(0)
+        a_copy(1, SCALAR)
+        r_interleave(0, VECTOR)
+        n_transpose(0, 0)
+        a_copy(0, SCALAR)
+        dh_matmul(1, 0)
+        dh_matmul(2, 0)
+        g_interleave(3, 0, 3, SCALAR)
+        g_interleave(3, 3, 4, VECTOR)
+        dh_matmul(2, 1)
+        dh_matmul(2, 3)
+        r_quantize(0)
+        a_quantize()
+        multiply(2, 0)
+        n_copy(0, 0, SCALAR)
+        dx_matmul(0, 1)
+        dh_matmul(2, 2)
+        multiply(2, 3)
+        dx_copy(0, 1, SCALAR)
+        dx_matmul(0, 0)
+        dx_matmul(0, 2)
+        multiply(2, 1)
+        x_sort(2, SCALAR)
+        dh_matmul(1, 2)
+        dh_matmul(1, 1)
+        multiply(2, 2)
+        n_transpose(2, 0)
+        g_quantize(3)
+        dx_copy(0, 2, SCALAR)
+        x_transpose(2, 0)
+        dx_copy(0, 0, SCALAR)
+        n_transpose(2, 1)
+        r_interleave(2, VECTOR)
+        dx_matmul(0, 3)
+        x_copy(2, 0, SCALAR)
+        dh_matmul(1, 3)
+        dx_copy(0, 3, SCALAR)
+        dh_matmul(3, 1)
+        multiply(1, 1)
+        n_copy(2, 1, SCALAR)
+        x_transpose(2, 1)
         dx_store(0, 0, J)
-        dh_mm(1, 0, 7)
-        x_pre(1, "V")
-        x_pre(2, "S")
-        r_quant(2)
-        x_tp(1, 1, 0)
-        mul(1, 2)
-        n_cp(2, 1, "S")
-        dx_mm(2, 1, 1)
-        x_cp(1, 1, "S")
-        mul(1, 1)
-        dx_mm(2, 0, 6)
-        dx_mm(2, 3, 2)
-        mul(1, 3)
-        dx_cp(2, 0, "S")
-        dx_mm(2, 2, 0)
-        x_tp(2, 0, 3)
-        mul(1, 0)
-        dx_cp(2, 1, "S")
-        dh_mm(3, 3, 4)
-        x_pre(3, "V")
-        dx_cp(2, 3, "S")
-        n_tp(1, 0, 6)
-        d_int(1, (0, 4), "V")
-        dx_cp(2, 2, "S")
-        n_tp(1, 1, 7)
-        x_cp(2, 0, "S")
-        x_tp(1, 0, 1)
+        r_quantize(2)
+        n_copy(2, 0, SCALAR)
+        multiply(1, 0)
+        dx_matmul(2, 3)
+        x_copy(2, 1, SCALAR)
+        dx_matmul(2, 1)
+        multiply(1, 2)
+        dx_matmul(2, 0)
+        dx_copy(2, 3, SCALAR)
+        dx_matmul(2, 2)
+        multiply(1, 3)
+        n_transpose(1, 0)
+        dx_copy(2, 0, SCALAR)
+        n_quantize(0)
+        x_transpose(0, 1)
+        dx_copy(2, 2, SCALAR)
+        n_transpose(1, 1)
+        r_interleave(1, VECTOR)
+        dx_copy(2, 1, SCALAR)
+        dh_matmul(3, 2)
+        dh_matmul(3, 0)
+        n_copy(1, 0, SCALAR)
         dx_store(2, 0, J)
-        dh_mm(3, 1, 2)
-        n_cp(1, 1, "S")
-        mul(3, 0)
-        dh_mm(3, 2, 0)
-        x_tp(3, 0, 3)
-        n_cp(1, 0, "S")
-        r_quant(1)
-        x_tp(2, 1, 7)
-        x_cp(3, 0, "S")
-        mul(3, 3)
-        dx_mm(1, 0, 5)
-        x_cp(2, 1, "S")
-        dx_mm(1, 1, 6)
-        mul(3, 1)
-        x_tp(0, 1, 3)
-        dx_cp(1, 0, "S")
-        mul(3, 2)
-        x_tp(3, 1, 4)
-        x_cp(1, 0, "S")
-        x_quant(3, 0)
-        dx_mm(1, 2, 7)
-        d_int(3, (0, 2), "V")
-        dx_cp(1, 1, "S")
-        dx_mm(1, 3, 2)
-        x_tp(0, 0, 5)
-        dx_cp(1, 2, "S")
-        d_int(3, (2, 4), "V")
-        n_tp(3, 0, 0)
-        dx_cp(1, 3, "S")
-        r_quant(3, 0)
-        n_tp(3, 1, 1)
-        r_quant(3, 1)
-        x_cp(0, 0, "S")
+        x_transpose(0, 0)
+        multiply(3, 2)
+        n_copy(1, 1, SCALAR)
+        dh_matmul(3, 3)
+        r_quantize(1)
+        x_copy(0, 0, SCALAR)
+        multiply(3, 0)
+        x_copy(0, 1, SCALAR)
+        dx_matmul(1, 0)
+        dx_matmul(1, 1)
+        multiply(3, 3)
+        dx_copy(1, 0, SCALAR)
+        dx_matmul(1, 3)
+        dx_matmul(1, 2)
+        multiply(3, 1)
+        dx_copy(1, 1, SCALAR)
+        x_transpose(1, 1)
+        x_quantize(0)
+        dx_copy(1, 2, SCALAR)
+        x_transpose(1, 0)
+        n_transpose(3, 1)
+        dx_copy(1, 3, SCALAR)
+        r_interleave(3, VECTOR, 0)
+        da_matmul(0, 0)
+        x_copy(1, 1, SCALAR)
         dx_store(1, 0, J)
-        x_quant(2)
-        dx_mm(3, 2, 6)
-        x_cp(0, 1, "S")
-        dx_mm(3, 0, 7)
-        n_quant(2)
-        dx_mm(3, 1, 2)
-        n_cp(3, 0, "S")
-        dx_cp(3, 0, "V")
-        da_mm(2, 2, 5)
-        dx_cp(3, 1, "S")
-        dx_mm(3, 3, 3)
-        x_quant(0)
-        da_mm(2, 0, 0)
-        n_cp(3, 1, "S")
-        da_mm(2, 3, 7)
-        dx_store(3, 0, 2)
-        x_quant(1)
-        da_mm(2, 1, 2)
-        dx_cp(3, 2, "S")
-        da_mm(0, 0)
-        n_quant(1)
-        da_mm(0, 1)
-        dx_cp(3, 3, "S")
-        da_mm(0, 3)
-        n_quant(3, 1)
-        da_mm(1, 0)
-        x_cp(3, 1, "S")
-        n_quant(3, 0)
+        r_interleave(3, VECTOR, 1)
+        da_matmul(0, 3)
+        n_transpose(3, 0)
+        n_copy(3, 1, SCALAR)
+        r_quantize(3, 0)
+        da_matmul(0, 2)
+        r_quantize(3, 1)
+        x_copy(1, 0, SCALAR)
+        da_matmul(0, 1)
+        x_sort(3, VECTOR)
+        dx_matmul(3, 3)
+        n_copy(3, 0, SCALAR)
+        dx_matmul(3, 2)
+        n_quantize(1)
+        x_transpose(3, 0)
+        dx_copy(3, 3, SCALAR)
+        x_transpose(3, 1)
+        x_quantize(1)
+        dx_copy(3, 2, SCALAR)
+        dx_matmul(3, 0)
+        x_quantize(2)
+        da_matmul(1, 1)
+        x_copy(3, 0, SCALAR)
         dx_store(3, 2, 4)
-        da_mm(1, 1)
-        da_mm(3, 1)
-        x_quant(3, 1)
-        da_mm(1, 3)
-        da_cp(1, "S")
-        da_mm(3, 0)
-        da_mm(3, 3)
-        da_mm(1, 2)
-        da_cp(0, "S")
-        da_store(1)
-        da_cp(3, "V")
-        da_mm(3, 2)
-        da_mm(0, 2)
-        da_store(0)
-        da_store(3)
-        da_cp(2, "S")
-        da_store(2)
+        dx_matmul(3, 1)
+        n_quantize(2)
+        da_matmul(1, 2)
+        dx_copy(3, 0, SCALAR)
+        da_matmul(1, 3)
+        x_quantize(3, 0)
+        dx_copy(3, 1, SCALAR)
+        da_matmul(2, 0)
+        n_quantize(3, 1)
+        da_matmul(1, 0)
+        n_quantize(3, 0)
+        x_copy(3, 1, SCALAR)
+        da_matmul(2, 1)
+        dx_store(3, 0, 2)
+        da_matmul(3, 0)
+        da_matmul(3, 1)
+        x_quantize(3, 1)
+        da_copy(0, 0, SCALAR)
+        da_matmul(2, 2)
+        da_copy(1, 0, SCALAR)
+        da_matmul(3, 2)
+        da_copy(0, 1, VECTOR)
+        da_store(0, 0)
+        da_matmul(3, 3)
+        da_copy(1, 1, VECTOR)
+        da_store(1, 0)
+        da_copy(2, 0, SCALAR)
+        da_store(0, 1)
+        da_matmul(2, 3)
+        da_store(1, 1)
+        da_copy(2, 1, SCALAR)
+        da_store(2, 0)
+        da_copy(3, 0, VECTOR)
+        da_store(2, 1)
+        da_copy(3, 1, VECTOR)
+        da_store(3, 0)
+        da_store(3, 1)

from contextlib import ExitStack

import concourse.mybir as mybir
from concourse.masks import make_identity

SAMPLES, D, CO, R = 16, 512, 128, 512
TOKENS = SAMPLES * CO
FLOPS = 3 * 2 * D * R * TOKENS
BYTES = 2 * (2 * D * TOKENS + 2 * D * R) + 4 * (R * TOKENS + D * TOKENS + D * R)

P = 128
J = 4
B = 4
G = SAMPLES // B
NT = B * CO
BANKS = 8
BANK = 512

X_SORTED_ON_ENGINE = (2, 3)

F32 = mybir.dt.float32
BF16 = mybir.dt.bfloat16
U32 = mybir.dt.uint32
U8 = mybir.dt.uint8
E4M3 = mybir.dt.float8_e4m3fn_x4
E5M2 = mybir.dt.float8_e5m2_x4

VECTOR, SCALAR = "vector", "scalar"


def tile_cptensorproduct_pa_v_kernel(tc, x1, A, t2, w, C, t3, grad_out, out_0, out_1):
    nc = tc.nc
    with ExitStack() as ctx:
        keep = ctx.enter_context(tc.tile_pool(name="keep", bufs=1))
        ring = ctx.enter_context(tc.tile_pool(name="ring", bufs=2))
        psum = ctx.enter_context(tc.psum_pool(name="psum", bufs=1))
        ctx.enter_context(tc.manual_schedule())


        def by_sample(name, dtype):
            return keep.tile([P, B, J, CO], dtype, name=name, align_bytes=64)

        g_raw = [by_sample("g_raw%d" % i, BF16) for i in range(G)]
        t3_raw = [by_sample("t3_raw%d" % i, F32) for i in range(G)]
        x_raw = [
            by_sample("x_raw%d" % i, BF16)
            if i in X_SORTED_ON_ENGINE
            else keep.tile([P, J, B, CO], BF16, name="x_raw%d" % i, align_bytes=64)
            for i in range(G)
        ]
        c_raw = keep.tile([P, J, R], BF16, name="c_raw", align_bytes=64)
        a_raw = keep.tile([P, J, R], BF16, name="a_raw", align_bytes=64)

        def load_matrix(tile, matrix):
            nc.sync.dma_start(out=tile[:], in_=matrix.rearrange("(p j) r -> p j r", j=J))

        def load_samples(tile, tensor, i, b0, b1):
            nc.sync.dma_start(
                out=tile[:, b0:b1].rearrange("p b j c -> p b (j c)"),
                in_=tensor[B * i + b0 : B * i + b1].rearrange("b (p j) c -> p b (j c)", j=J),
            )

        def load_t3_half(h):
            rows = slice(2 * h, 2 * h + 2)
            view = t3[0:B].rearrange("b (p j) c -> p b j c", j=J)
            nc.sync.dma_start(out=t3_raw[0][:, :, rows, :], in_=view[:, :, rows, :])

        def load_x(i):
            if i in X_SORTED_ON_ENGINE:
                load_samples(x_raw[i], x1, i, 0, B)
            else:
                for b in range(B):
                    nc.sync.dma_start(
                        out=x_raw[i][:, :, b, :], in_=x1[B * i + b].rearrange("(p j) c -> p j c", j=J)
                    )

        load_matrix(c_raw, C)
        load_samples(g_raw[0], grad_out, 0, 3, 4)
        load_samples(g_raw[0], grad_out, 0, 2, 3)
        load_samples(g_raw[2], grad_out, 2, 0, B)
        load_samples(g_raw[0], grad_out, 0, 1, 2)
        load_samples(g_raw[0], grad_out, 0, 0, 1)
        load_samples(g_raw[1], grad_out, 1, 0, B)
        load_t3_half(1)
        load_t3_half(0)
        load_matrix(a_raw, A)
        load_samples(g_raw[3], grad_out, 3, 0, B)
        load_samples(t3_raw[2], t3, 2, 0, B)
        load_x(2)
        load_samples(t3_raw[1], t3, 1, 0, B)
        load_x(0)
        load_samples(t3_raw[3], t3, 3, 0, B)
        load_x(1)
        load_x(3)

        identity = keep.tile([P, P], F32, name="identity")
        make_identity(nc, identity[:])


        empty = list(range(BANKS))

        def open_bank():
            k = empty[0]
            empty.remove(k)
            return k, psum.tile([P, BANK], F32, name="bank%d" % k)

        def copy(engine, out, in_):
            if engine == VECTOR:
                nc.vector.tensor_copy(out=out, in_=in_)
            else:
                nc.scalar.copy(out=out, in_=in_)

        def copy_from_bank(engine, out, bank, in_):
            copy(engine, out, in_)
            empty.append(bank[0])

        def operand(name):
            return (
                keep.tile([P, 512], U32, name=name + "_codes", align_bytes=64),
                keep.tile([P, 512], U8, name=name + "_scales", align_bytes=64),
            )

        def quantize(op, grouped, fmt, half=None):
            n0, n1 = (0, 512) if half is None else (256 * half, 256 * (half + 1))
            nc.vector.quantize_mx(
                out=op[0][:, n0:n1].bitcast(fmt), scales=op[1][:, n0:n1], in_=grouped[:, J * n0 : J * n1]
            )

        def multiply_mx(out, stationary, column_tile, stationary_fmt, moving, moving_fmt, start, stop):
            cols = slice(P * column_tile, P * (column_tile + 1))
            nc.tensor.matmul_mx(
                out=out[:],
                lhsT=stationary[0][:, cols].bitcast(stationary_fmt),
                lhsT_scale=stationary[1][:, cols],
                rhs=moving[0][:].bitcast(moving_fmt),
                rhs_scale=moving[1][:],
                start=start,
                stop=stop,
            )

        def transpose_words(words, word_step, half, bank):
            for s in range(2):
                for u in range(2):
                    first = 256 * (2 * half + s) + (u if word_step == 2 else P * u)
                    block = words[:, first : first + word_step * (P - 1) + 1 : word_step]
                    nc.tensor.transpose(bank[1][:, P * (2 * s + u) : P * (2 * s + u + 1)], block, identity[:])

        def copy_words(engine, grouped, half, bank):
            copy_from_bank(
                engine,
                grouped[:].bitcast(F32)[:, BANK * half : BANK * (half + 1)].rearrange("p (s k u) -> p s k u", s=2, u=2),
                bank,
                bank[1][:].rearrange("p (s u k) -> p s k u", s=2, u=2),
            )


        c_op = operand("c")
        c_grouped = keep.tile([P, R * J], BF16, name="c_grouped", align_bytes=64)

        def c_interleave(half, engine):
            copy(
                engine,
                c_grouped[:].rearrange("p (t m j) -> p t m j", t=J, j=J)[:, :, 64 * half : 64 * (half + 1), :],
                c_raw[:, :, 256 * half : 256 * (half + 1)].rearrange("p j (m t) -> p t m j", t=J),
            )

        def c_quantize():
            quantize(c_op, c_grouped, E4M3)

        g_op = [operand("g%d" % i) for i in range(G)]
        g_grouped = {}

        def g_interleave(i, b0, b1, engine):
            if i not in g_grouped:
                g_grouped[i] = ring.tile([P, NT, J], BF16, name="g_grouped", align_bytes=64, bufs=3)
            copy(
                engine,
                g_grouped[i][:, CO * b0 : CO * b1, :].rearrange("p (b c k) j -> p b c j k", b=b1 - b0, k=4),
                g_raw[i][:, b0:b1].rearrange("p b j (c k) -> p b c j k", k=4),
            )

        def g_quantize(i, half=None):
            quantize(g_op[i], g_grouped[i][:].rearrange("p n j -> p (n j)"), E5M2, half)


        dh = {}
        dt1 = {}

        def dh_matmul(i, t):
            dh[i, t] = open_bank()
            multiply_mx(dh[i, t][1], c_op, t, E4M3, g_op[i], E5M2, True, True)

        def multiply(i, t):
            if i not in dt1:
                dt1[i] = ring.tile([P, J, NT], BF16, name="dt1", align_bytes=64)
            nc.vector.tensor_tensor(
                out=dt1[i][:, t, :].rearrange("p (b c) -> p b c", b=B),
                in0=dh[i, t][1][:].rearrange("p (b c) -> p b c", b=B),
                in1=t3_raw[i][:, :, t, :],
                op=mybir.AluOpType.mult,
            )
            empty.append(dh[i, t][0])

        r_op = [operand("r%d" % i) for i in range(G)]
        r_grouped = {}

        def r_interleave(i, engine, half=None):
            if i not in r_grouped:
                r_grouped[i] = ring.tile([P, NT, J], BF16, name="r_grouped", align_bytes=64)
            n0, n1 = (0, NT) if half is None else (256 * half, 256 * (half + 1))
            copy(
                engine,
                r_grouped[i][:, n0:n1, :].rearrange("p (c k) t -> p c t k", k=4),
                dt1[i][:, :, n0:n1].rearrange("p t (c k) -> p c t k", k=4),
            )

        def r_quantize(i, half=None):
            quantize(r_op[i], r_grouped[i][:].rearrange("p n t -> p (n t)"), E5M2, half)

        n_op = [operand("n%d" % i) for i in range(G)]
        n_bank = {}
        n_grouped = {}

        def n_transpose(i, half):
            n_bank[i, half] = open_bank()
            transpose_words(dt1[i][:].rearrange("p t n -> p (t n)").bitcast(F32), 2, half, n_bank[i, half])

        def n_copy(i, half, engine):
            if i not in n_grouped:
                n_grouped[i] = keep.tile([P, J * R], BF16, name="n_grouped%d" % i, align_bytes=64)
            copy_words(engine, n_grouped[i], half, n_bank[i, half])

        def n_quantize(i, half=None):
            quantize(n_op[i], n_grouped[i], E5M2, half)


        x_op = [operand("x%d" % i) for i in range(G)]
        x_sorted = {}
        x_bank = {}
        x_grouped = {}

        def x_sort(i, engine):
            x_sorted[i] = ring.tile([P, J * NT // 2], F32, name="x_sorted", align_bytes=64)
            words = x_raw[i][:].rearrange("p b j c -> p (b j c)").bitcast(F32)
            copy(
                engine,
                x_sorted[i][:].rearrange("p (j u b q) -> p j u b q", j=J, u=2, b=B),
                words.rearrange("p (b j q u) -> p j u b q", b=B, j=J, u=2),
            )

        def x_transpose(i, half):
            x_bank[i, half] = open_bank()
            if i in X_SORTED_ON_ENGINE:
                transpose_words(x_sorted[i], 1, half, x_bank[i, half])
            else:
                transpose_words(x_raw[i][:].rearrange("p j b c -> p (j b c)").bitcast(F32), 2, half, x_bank[i, half])

        def x_copy(i, half, engine):
            if i not in x_grouped:
                x_grouped[i] = keep.tile([P, J * D], BF16, name="x_grouped%d" % i, align_bytes=64)
            copy_words(engine, x_grouped[i], half, x_bank[i, half])

        def x_quantize(i, half=None):
            quantize(x_op[i], x_grouped[i], E4M3, half)


        a_op = operand("a")
        a_bank = {}
        a_grouped = keep.tile([P, J * D], BF16, name="a_grouped", align_bytes=64)

        def a_transpose(half):
            a_bank[half] = open_bank()
            transpose_words(a_raw[:].rearrange("p j r -> p (j r)").bitcast(F32), 2, half, a_bank[half])

        def a_copy(half, engine):
            copy_words(engine, a_grouped, half, a_bank[half])

        def a_quantize():
            quantize(a_op, a_grouped, E4M3)


        dx = {}
        dx_rows = {}

        def dx_matmul(i, j):
            dx[i, j] = open_bank()
            multiply_mx(dx[i, j][1], a_op, j, E4M3, r_op[i], E5M2, True, True)

        def dx_copy(i, j, engine):
            if i not in dx_rows:
                dx_rows[i] = ring.tile([P, B, J, CO], F32, name="dx_rows", align_bytes=64, bufs=3)
            copy_from_bank(engine, dx_rows[i][:, :, j, :], dx[i, j], dx[i, j][1][:].rearrange("p (b c) -> p b c", b=B))

        def dx_store(i, j0, j1):
            nc.sync.dma_start(
                out=out_0[B * i : B * (i + 1)].rearrange("b (p j) c -> p b j c", j=J)[:, :, j0:j1, :],
                in_=dx_rows[i][:, :, j0:j1, :],
            )


        da = {}
        da_passes = {}
        da_rows = keep.tile([P, J, R], F32, name="da_rows", align_bytes=64)
        da_view = out_1.rearrange("(p j) r -> p j r", j=J)

        def da_matmul(i, j):
            if j not in da:
                da[j] = open_bank()
                da_passes[j] = 0
            da_passes[j] += 1
            multiply_mx(da[j][1], x_op[i], j, E4M3, n_op[i], E5M2, da_passes[j] == 1, da_passes[j] == G)

        def da_copy(j, half, engine):
            copy(
                engine,
                da_rows[:, j, 256 * half : 256 * (half + 1)].rearrange("p (m t) -> p m t", t=J),
                da[j][1][:].rearrange("p (t m) -> p m t", t=J)[:, 64 * half : 64 * (half + 1), :],
            )

        def da_store(j, half):
            cols = slice(256 * half, 256 * (half + 1))
            nc.sync.dma_start(out=da_view[:, j, cols], in_=da_rows[:, j, cols])

        c_interleave(0, VECTOR)
        c_interleave(1, SCALAR)
        g_interleave(0, 2, 3, VECTOR)
        g_interleave(0, 3, 4, VECTOR)
        c_quantize()
        g_interleave(2, 0, 3, SCALAR)
        g_interleave(0, 1, 2, VECTOR)
        g_interleave(0, 0, 1, VECTOR)
        g_quantize(0, 1)
        g_quantize(0, 0)
        g_interleave(2, 3, 4, VECTOR)
        dh_matmul(0, 2)
        g_interleave(1, 0, 3, SCALAR)
        g_quantize(2)
        dh_matmul(0, 3)
        multiply(0, 2)
        dh_matmul(0, 1)
        multiply(0, 3)
        dh_matmul(0, 0)
        g_interleave(1, 3, 4, SCALAR)
        multiply(0, 1)
        n_transpose(0, 1)
        multiply(0, 0)
        n_copy(0, 1, SCALAR)
        a_transpose(1)
        g_quantize(1)
        a_transpose(0)
        a_copy(1, SCALAR)
        r_interleave(0, VECTOR)
        n_transpose(0, 0)
        a_copy(0, SCALAR)
        dh_matmul(1, 0)
        dh_matmul(2, 0)
        g_interleave(3, 0, 3, SCALAR)
        g_interleave(3, 3, 4, VECTOR)
        dh_matmul(2, 1)
        dh_matmul(2, 3)
        r_quantize(0)
        a_quantize()
        multiply(2, 0)
        n_copy(0, 0, SCALAR)
        dx_matmul(0, 1)
        dh_matmul(2, 2)
        multiply(2, 3)
        dx_copy(0, 1, SCALAR)
        dx_matmul(0, 0)
        dx_matmul(0, 2)
        multiply(2, 1)
        x_sort(2, SCALAR)
        dh_matmul(1, 2)
        dh_matmul(1, 1)
        multiply(2, 2)
        n_transpose(2, 0)
        g_quantize(3)
        dx_copy(0, 2, SCALAR)
        x_transpose(2, 0)
        dx_copy(0, 0, SCALAR)
        n_transpose(2, 1)
        r_interleave(2, VECTOR)
        dx_matmul(0, 3)
        x_copy(2, 0, SCALAR)
        dh_matmul(1, 3)
        dx_copy(0, 3, SCALAR)
        dh_matmul(3, 1)
        multiply(1, 1)
        n_copy(2, 1, SCALAR)
        x_transpose(2, 1)
        dx_store(0, 0, J)
        r_quantize(2)
        n_copy(2, 0, SCALAR)
        multiply(1, 0)
        dx_matmul(2, 3)
        x_copy(2, 1, SCALAR)
        dx_matmul(2, 1)
        multiply(1, 2)
        dx_matmul(2, 0)
        dx_copy(2, 3, SCALAR)
        dx_matmul(2, 2)
        multiply(1, 3)
        n_transpose(1, 0)
        dx_copy(2, 0, SCALAR)
        n_quantize(0)
        x_transpose(0, 1)
        dx_copy(2, 2, SCALAR)
        n_transpose(1, 1)
        r_interleave(1, VECTOR)
        dx_copy(2, 1, SCALAR)
        dh_matmul(3, 2)
        dh_matmul(3, 0)
        n_copy(1, 0, SCALAR)
        dx_store(2, 0, J)
        x_transpose(0, 0)
        multiply(3, 2)
        n_copy(1, 1, SCALAR)
        dh_matmul(3, 3)
        r_quantize(1)
        x_copy(0, 0, SCALAR)
        multiply(3, 0)
        x_copy(0, 1, SCALAR)
        dx_matmul(1, 0)
        dx_matmul(1, 1)
        multiply(3, 3)
        dx_copy(1, 0, SCALAR)
        dx_matmul(1, 3)
        dx_matmul(1, 2)
        multiply(3, 1)
        dx_copy(1, 1, SCALAR)
        x_transpose(1, 1)
        x_quantize(0)
        dx_copy(1, 2, SCALAR)
        x_transpose(1, 0)
        n_transpose(3, 1)
        dx_copy(1, 3, SCALAR)
        r_interleave(3, VECTOR, 0)
        da_matmul(0, 0)
        x_copy(1, 1, SCALAR)
        dx_store(1, 0, J)
        r_interleave(3, VECTOR, 1)
        da_matmul(0, 3)
        n_transpose(3, 0)
        n_copy(3, 1, SCALAR)
        r_quantize(3, 0)
        da_matmul(0, 2)
        r_quantize(3, 1)
        x_copy(1, 0, SCALAR)
        da_matmul(0, 1)
        x_sort(3, VECTOR)
        dx_matmul(3, 3)
        n_copy(3, 0, SCALAR)
        dx_matmul(3, 2)
        n_quantize(1)
        x_transpose(3, 0)
        dx_copy(3, 3, SCALAR)
        x_transpose(3, 1)
        x_quantize(1)
        dx_copy(3, 2, SCALAR)
        dx_matmul(3, 0)
        x_quantize(2)
        da_matmul(1, 1)
        x_copy(3, 0, SCALAR)
        dx_store(3, 2, 4)
        dx_matmul(3, 1)
        n_quantize(2)
        da_matmul(1, 2)
        dx_copy(3, 0, SCALAR)
        da_matmul(1, 3)
        x_quantize(3, 0)
        dx_copy(3, 1, SCALAR)
        da_matmul(2, 0)
        n_quantize(3, 1)
        da_matmul(1, 0)
        n_quantize(3, 0)
        x_copy(3, 1, SCALAR)
        da_matmul(2, 1)
        dx_store(3, 0, 2)
        da_matmul(3, 0)
        da_matmul(3, 1)
        x_quantize(3, 1)
        da_copy(0, 0, SCALAR)
        da_matmul(2, 2)
        da_copy(1, 0, SCALAR)
        da_matmul(3, 2)
        da_copy(0, 1, VECTOR)
        da_store(0, 0)
        da_matmul(3, 3)
        da_copy(1, 1, VECTOR)
        da_store(1, 0)
        da_copy(2, 0, SCALAR)
        da_store(0, 1)
        da_matmul(2, 3)
        da_store(1, 1)
        da_copy(2, 1, SCALAR)
        da_store(2, 0)
        da_copy(3, 0, VECTOR)
        da_store(2, 1)
        da_copy(3, 1, VECTOR)
        da_store(3, 0)
        da_store(3, 1)
